import numpy as np
import ml_dtypes


def mxq(x, axis, fmt="e4m3"):
    dtype, down = {"e4m3": (ml_dtypes.float8_e4m3fn, 7), "e5m2": (ml_dtypes.float8_e5m2, 14)}[fmt]
    v = np.moveaxis(np.asarray(x, np.float32).astype(ml_dtypes.bfloat16).astype(np.float64), axis, -1)
    blocks = v.reshape(v.shape[:-1] + (-1, 32))
    amax = np.abs(blocks).max(-1, keepdims=True)
    byte = np.maximum(np.where(amax > 0, np.frexp(amax)[1] - 1 + 127, 0) - down, 1)
    scale = np.exp2(byte - 127.0)
    codes = (blocks / scale).astype(np.float32).astype(dtype).astype(np.float64)
    return np.moveaxis((codes * scale).reshape(v.shape), -1, axis)


WIDE = False


def mx_kscale(k):
    if not WIDE:
        return np.ones(k)
    levels = np.array([10, -10, 5, -5, 0])
    a = np.random.permutation(np.resize(levels, k // 512 * 4)).reshape(k // 512, 4)
    idx = np.arange(k)
    return np.exp2(a[idx // 512, idx % 128 // 32])


BF16 = ml_dtypes.bfloat16


def bf(x):
    return np.asarray(x, np.float32).astype(BF16)


def f64(x):
    return np.asarray(x).astype(np.float64)


B, H, HKV, S, D = 1, 16, 2, 1024, 128
G = H // HKV
NEG = -1e9


def setup_inputs():
    s = mx_kscale(S)
    keep = np.random.random((B, 1, S, S)) < 0.75
    return {"query": bf(np.random.standard_normal((B, H, S, D))),
            "key": bf(np.random.standard_normal((B, HKV, S, D))),
            "value": bf(np.random.standard_normal((B, HKV, S, D)) * 0.25 * np.sqrt(S) * s.max() / s[:, None]),
            "attention_mask": bf(np.where(keep, 0.5 * np.random.standard_normal((B, 1, S, S)) + np.log(s), NEG)),
            "sinks": bf(np.log(S * s.max()) - 3.5 + np.random.standard_normal(H))}


def reference(query, key, value, attention_mask, sinks):
    scaling = 1.0 / np.sqrt(D)
    k = np.repeat(f64(key), G, axis=1)
    attn = (f64(query) @ k.transpose(0, 1, 3, 2)) * scaling
    attn = attn + f64(attention_mask)[:, :, :, :attn.shape[-1]]
    sink_col = np.broadcast_to(f64(sinks).reshape(1, H, 1, 1), (B, H, S, 1))
    combined = np.concatenate([attn, sink_col], axis=-1)
    combined = combined - combined.max(-1, keepdims=True)
    e = np.exp(combined[..., :-1])
    den = e.sum(-1, keepdims=True) + np.exp(combined[..., -1:])
    eg = e.reshape(B, HKV, G * S, S)
    pv = mxq(eg, 3, "e4m3") @ mxq(f64(value), 2, "e4m3")
    out = pv.reshape(B, H, S, D) / den
    return out.transpose(0, 2, 1, 3)

@@ -1,0 +1,266 @@
+from contextlib import ExitStack
+
+import concourse.mybir as mybir
+from concourse.masks import make_identity
+
+F32 = mybir.dt.float32
+BF16 = mybir.dt.bfloat16
+U32 = mybir.dt.uint32
+U8 = mybir.dt.uint8
+FP8X4 = mybir.dt.float8_e4m3fn_x4
+ACT = mybir.ActivationFunctionType
+ALU = mybir.AluOpType
+AX = mybir.AxisListType
+
+P = 128
+H = 16
+HKV = 2
+S = 1024
+D = 128
+NT = S // P
+NU = H * NT
+SCALE = 1.0 / (D ** 0.5)
+FLOPS = 2 * 2 * H * S * S * D
+
+
+def tile_deepseekv4attention_kernel(tc, query, key, value, attention_mask, sinks, out):
+    nc = tc.nc
+    with ExitStack() as ctx:
+        const = ctx.enter_context(tc.tile_pool(name="const", bufs=1))
+        qt_pool = ctx.enter_context(tc.tile_pool(name="qtp", bufs=3))
+        e_pool = ctx.enter_context(tc.tile_pool(name="ep", bufs=3))
+        et_pool = ctx.enter_context(tc.tile_pool(name="etp", bufs=3))
+        c_pool = ctx.enter_context(tc.tile_pool(name="cp", bufs=10))
+        small = ctx.enter_context(tc.tile_pool(name="small", bufs=4))
+        o_pool = ctx.enter_context(tc.tile_pool(name="op", bufs=3))
+        ps_s = ctx.enter_context(tc.psum_pool(name="ps_s", bufs=4))
+        ps_t = ctx.enter_context(tc.psum_pool(name="ps_t", bufs=2))
+        ps_o = ctx.enter_context(tc.psum_pool(name="ps_o", bufs=1))
+        ps_q = ctx.enter_context(tc.psum_pool(name="ps_q", bufs=1))
+        ctx.enter_context(tc.manual_schedule())
+
+        q_v = query[0].rearrange("h (p t) d -> p h t d", t=NT)
+        m_v = attention_mask[0, 0].rearrange("(p t) k -> p t k", t=NT)
+        k_v = key[0].rearrange("g (a p) d -> p g a d", p=P)
+        v_v = value[0].rearrange("g (a p) d -> p g a d", p=P)
+        o_v = out[0].rearrange("(p t) h d -> p t h d", t=NT)
+
+        q_raw = const.tile([P, H, NT, D], BF16)
+        mask_sb = const.tile([P, NT, S], BF16)
+        k_raw = const.tile([P, HKV, NT, D], BF16)
+        v_raw = const.tile([P, HKV, NT, D], BF16)
+        sink_bf = const.tile([P, H], BF16)
+        kt_sb = const.tile([P, HKV, S], BF16)
+        v_codes = const.tile([P, HKV, 2 * D], U32, align_bytes=64)
+        v_scales = const.tile([P, HKV, 2 * D], U8, align_bytes=64)
+        ident = const.tile([P, P], BF16)
+        s_bufs = [const.tile([P, S + 8], F32, name="s_buf%d" % j) for j in range(4)]
+
+        make_identity(nc, ident[:])
+
+        nc.scalar.dma_start(out=sink_bf[:], in_=sinks.partition_broadcast(P))
+        nc.sync.dma_start(out=k_raw[:, 0], in_=k_v[:, 0])
+        for h in range(4):
+            nc.sync.dma_start(out=q_raw[:, h], in_=q_v[:, h])
+        nc.sync.dma_start(out=mask_sb[:, 0, :], in_=m_v[:, 0, :])
+        nc.sync.dma_start(out=v_raw[:, 0], in_=v_v[:, 0])
+        nc.sync.dma_start(out=mask_sb[:, 1, :], in_=m_v[:, 1, :])
+        nc.sync.dma_start(out=mask_sb[:, 2:4, :], in_=m_v[:, 2:4, :])
+        nc.sync.dma_start(out=mask_sb[:, 4:8, :], in_=m_v[:, 4:8, :])
+        for h in range(4, 8):
+            nc.sync.dma_start(out=q_raw[:, h], in_=q_v[:, h])
+        nc.sync.dma_start(out=k_raw[:, 1], in_=k_v[:, 1])
+        nc.sync.dma_start(out=v_raw[:, 1], in_=v_v[:, 1])
+        for h in range(8, H):
+            nc.sync.dma_start(out=q_raw[:, h], in_=q_v[:, h])
+
+        def prep_kt(g):
+            kt_ps = ps_q.tile([P, NT, P], BF16, tag="qt")
+            for a in range(NT):
+                nc.tensor.transpose(out=kt_ps[:, a, :], in_=k_raw[:, g, a, :], identity=ident[:])
+            nc.scalar.copy(out=kt_sb[:, g, :], in_=kt_ps[:].rearrange("p a k -> p (a k)"))
+
+        def prep_v(g):
+            vg = et_pool.tile([P, 2, D, 4], BF16, tag="vg", align_bytes=64)
+            nc.vector.tensor_copy(out=vg[:], in_=v_raw[:, g].rearrange("p (c t) d -> p c d t", t=4))
+            nc.vector.quantize_mx(
+                out=v_codes[:, g, :].bitcast(FP8X4),
+                scales=v_scales[:, g, :],
+                in_=vg[:].rearrange("p c d t -> p (c d t)"),
+            )
+
+        qt_sb = {}
+        qt_ps = {}
+
+        def prep_qt_pe(b):
+            hq, tp = divmod(b, 4)
+            q_ps = ps_q.tile([P, 8, P], BF16, tag="qt")
+            for t2 in range(2):
+                for j in range(4):
+                    nc.tensor.transpose(
+                        out=q_ps[:, t2 * 4 + j, :],
+                        in_=q_raw[:, 4 * hq + j, 2 * tp + t2, :],
+                        identity=ident[:],
+                    )
+            qt_ps[b] = q_ps
+
+        def prep_qt_copy(b):
+            qt = qt_pool.tile([P, 8, P], BF16, tag="qtsb")
+            nc.scalar.copy(out=qt[:], in_=qt_ps[b][:])
+            qt_sb[b] = qt
+
+        sc = {}
+        negm = {}
+        den = {}
+        rden = {}
+        e_sb = {}
+        tr_ps = {}
+        et_sb = {}
+        codes = {}
+        scales = {}
+        pv = {}
+
+        def where(i):
+            hq, r = divmod(i, 4 * NT)
+            t, j = divmod(r, 4)
+            return hq, t, j
+
+        def qk(i):
+            hq, t, j = where(i)
+            g = (4 * hq + j) // (H // HKV)
+            halves = []
+            for half in range(2):
+                sc_t = ps_s.tile([P, 512], F32, tag="sc", name="sc_t")
+                nc.tensor.matmul(
+                    out=sc_t[:],
+                    lhsT=qt_sb[i // 8][:, i % 8, :],
+                    rhs=kt_sb[:, g, 512 * half : 512 * half + 512],
+                    start=True,
+                    stop=True,
+                )
+                halves.append(sc_t)
+            sc[i] = halves
+
+        def p1p2(i):
+            hq, t, j = where(i)
+            s_t = s_bufs[j]
+            if t == 0:
+                nc.vector.tensor_copy(out=s_t[:, S : S + 1], in_=sink_bf[:, 4 * hq + j : 4 * hq + j + 1])
+            for half in range(2):
+                cols = slice(512 * half, 512 * half + 512)
+                nc.vector.scalar_tensor_tensor(
+                    out=s_t[:, cols],
+                    in0=sc[i][half][:],
+                    scalar=SCALE,
+                    in1=mask_sb[:, t, cols],
+                    op0=ALU.mult,
+                    op1=ALU.add,
+                )
+            nm = small.tile([P, 1], F32, tag="negm")
+            nc.vector.tensor_reduce(out=nm[:], in_=s_t[:, 0 : S + 1], axis=AX.X, op=ALU.max, negate=True)
+            negm[i] = nm
+
+        def p3(i):
+            hq, t, j = where(i)
+            if j == 0:
+                den_t = small.tile([P, 4], F32, tag="den")
+                den[i // 4] = den_t
+            e_t = e_pool.tile([P, S + 32], BF16, tag="e")
+            nc.scalar.activation(
+                out=e_t[:, 0 : S + 1],
+                in_=s_bufs[j][:, 0 : S + 1],
+                func=ACT.Exp,
+                bias=negm[i][:],
+                scale=1.0,
+                accum_out=den[i // 4][:, j : j + 1],
+            )
+            e_sb[i] = e_t
+
+        def tr(i):
+            tr_t = ps_t.tile([P, 8, P], BF16, tag="tr")
+            for a in range(8):
+                nc.tensor.transpose(out=tr_t[:, a, :], in_=e_sb[i][:, P * a : P * a + P], identity=ident[:])
+            tr_ps[i] = tr_t
+
+        def p4(i):
+            et_t = et_pool.tile([P, 2, P, 4], BF16, tag="et", align_bytes=64)
+            nc.scalar.copy(out=et_t[:], in_=tr_ps[i][:].rearrange("p (c t) q -> p c q t", t=4))
+            et_sb[i] = et_t
+
+        def p5(i):
+            c_t = c_pool.tile([P, 2 * P], U32, tag="codes", align_bytes=64)
+            sc_b = c_pool.tile([P, 2 * P], U8, tag="scales", align_bytes=64)
+            nc.vector.quantize_mx(
+                out=c_t[:].bitcast(FP8X4),
+                scales=sc_b[:],
+                in_=et_sb[i][:].rearrange("p c q t -> p (c q t)"),
+            )
+            codes[i] = c_t
+            scales[i] = sc_b
+
+        def mx(quad):
+            pv_t = ps_o.tile([P, 4, D], F32, tag="pv")
+            for j in range(4):
+                i = 4 * quad + j
+                hq = where(i)[0]
+                g = (4 * hq + j) // (H // HKV)
+                for c in range(2):
+                    cols = slice(P * c, P * c + P)
+                    nc.tensor.matmul_mx(
+                        out=pv_t[:, j, :],
+                        lhsT=codes[i][:, cols].bitcast(FP8X4),
+                        lhsT_scale=scales[i][:, cols],
+                        rhs=v_codes[:, g, cols].bitcast(FP8X4),
+                        rhs_scale=v_scales[:, g, cols],
+                        start=(c == 0),
+                        stop=(c == 1),
+                    )
+            pv[quad] = pv_t
+
+        def recip(quad):
+            r_t = small.tile([P, 4], F32, tag="rden")
+            nc.vector.reciprocal(out=r_t[:], in_=den[quad][:])
+            rden[quad] = r_t
+
+        def p6(quad):
+            hq, t, j0 = where(4 * quad)
+            o_t = o_pool.tile([P, 4, D], F32, tag="o")
+            for j in range(4):
+                nc.scalar.activation(
+                    out=o_t[:, j, :], in_=pv[quad][:, j, :], func=ACT.Copy, scale=rden[quad][:, j : j + 1]
+                )
+            nc.sync.dma_start(out=o_v[:, t, 4 * hq : 4 * hq + 4, :], in_=o_t[:])
+
+        prep_kt(0)
+        prep_qt_pe(0)
+        prep_qt_copy(0)
+        prep_v(0)
+
+        for i in range(-1, NU + 4):
+            quad_due = i - 3 >= 0 and (i - 3) % 4 == 3
+            quad = (i - 3) // 4
+            prep_b = (i + 3) // 8 if (i + 3) % 8 == 0 and 0 < (i + 3) // 8 < NU // 8 else None
+            if i + 1 < NU:
+                qk(i + 1)
+            if quad_due:
+                recip(quad)
+            if 0 <= i < NU:
+                p1p2(i)
+            if 0 <= i - 1 < NU:
+                p3(i - 1)
+            if quad_due:
+                mx(quad)
+            if 0 <= i - 1 < NU:
+                tr(i - 1)
+            if prep_b is not None:
+                prep_qt_pe(prep_b)
+            if 0 <= i - 2 < NU:
+                p4(i - 2)
+                p5(i - 2)
+            if quad_due:
+                p6(quad)
+            if prep_b is not None:
+                prep_qt_copy(prep_b)
+            if i == 40:
+                prep_kt(1)
+                prep_v(1)

@@ -20,6 +20,7 @@ D = 128
 NT = S // P
 NU = H * NT
 SCALE = 1.0 / (D ** 0.5)
+RSCALE = D ** 0.5
 FLOPS = 2 * 2 * H * S * S * D
 
 
@@ -54,9 +55,13 @@ def tile_deepseekv4attention_kernel(tc, query, key, value, attention_mask, sinks
         v_codes = const.tile([P, HKV, 2 * D], U32, align_bytes=64)
         v_scales = const.tile([P, HKV, 2 * D], U8, align_bytes=64)
         ident = const.tile([P, P], BF16)
-        s_bufs = [const.tile([P, S + 8], F32, name="s_buf%d" % j) for j in range(4)]
+        ident32 = const.tile([P, P], F32)
+        mask_t = const.tile([P, NT, NT, P], F32)
+        sink32 = const.tile([P, H], F32)
+        sinkc = const.tile([P, H], F32)
 
         make_identity(nc, ident[:])
+        make_identity(nc, ident32[:])
 
         nc.scalar.dma_start(out=sink_bf[:], in_=sinks.partition_broadcast(P))
         nc.sync.dma_start(out=k_raw[:, 0], in_=k_v[:, 0])
@@ -91,6 +96,16 @@ def tile_deepseekv4attention_kernel(tc, query, key, value, attention_mask, sinks
 
         qt_sb = {}
         qt_ps = {}
+        m_ps = {}
+
+        def prep_mask_pe(t):
+            mp = ps_q.tile([P, NT, P], BF16, tag="qt")
+            for a in range(NT):
+                nc.tensor.transpose(out=mp[:, a, :], in_=mask_sb[:, t, P * a : P * a + P], identity=ident[:])
+            m_ps[t] = mp
+
+        def prep_mask_copy(t):
+            nc.scalar.activation(out=mask_t[:, t], in_=m_ps[t][:], func=ACT.Copy, scale=RSCALE)
 
         def prep_qt_pe(b):
             hq, tp = divmod(b, 4)
@@ -136,43 +151,57 @@ def tile_deepseekv4attention_kernel(tc, query, key, value, attention_mask, sinks
                     lhsT=qt_sb[i // 8][:, i % 8, :],
                     rhs=kt_sb[:, g, 512 * half : 512 * half + 512],
                     start=True,
-                    stop=True,
+                    stop=False,
                 )
+                for a4 in range(4):
+                    nc.tensor.matmul(
+                        out=sc_t[:, P * a4 : P * a4 + P],
+                        lhsT=mask_t[:, t, 4 * half + a4, :],
+                        rhs=ident32[:],
+                        is_transpose=True,
+                        start=False,
+                        stop=(a4 == 3),
+                    )
                 halves.append(sc_t)
             sc[i] = halves
 
         def p1p2(i):
             hq, t, j = where(i)
-            s_t = s_bufs[j]
-            if t == 0:
-                nc.vector.tensor_copy(out=s_t[:, S : S + 1], in_=sink_bf[:, 4 * hq + j : 4 * hq + j + 1])
+            h = 4 * hq + j
+            mx2 = small.tile([P, 2], F32, tag="mx2")
             for half in range(2):
-                cols = slice(512 * half, 512 * half + 512)
-                nc.vector.scalar_tensor_tensor(
-                    out=s_t[:, cols],
-                    in0=sc[i][half][:],
-                    scalar=SCALE,
-                    in1=mask_sb[:, t, cols],
-                    op0=ALU.mult,
-                    op1=ALU.add,
-                )
+                nc.vector.tensor_reduce(out=mx2[:, half : half + 1], in_=sc[i][half][:], axis=AX.X, op=ALU.max)
+            mxx = small.tile([P, 1], F32, tag="mxx")
+            nc.vector.scalar_tensor_tensor(
+                out=mxx[:],
+                in0=mx2[:, 0:1],
+                scalar=mx2[:, 1:2],
+                in1=sinkc[:, h : h + 1],
+                op0=ALU.max,
+                op1=ALU.max,
+            )
             nm = small.tile([P, 1], F32, tag="negm")
-            nc.vector.tensor_reduce(out=nm[:], in_=s_t[:, 0 : S + 1], axis=AX.X, op=ALU.max, negate=True)
+            nc.vector.tensor_scalar(out=nm[:], in0=mxx[:], scalar1=-SCALE, scalar2=None, op0=ALU.mult)
             negm[i] = nm
 
         def p3(i):
             hq, t, j = where(i)
+            h = 4 * hq + j
             if j == 0:
-                den_t = small.tile([P, 4], F32, tag="den")
+                den_t = small.tile([P, 4, 3], F32, tag="den")
                 den[i // 4] = den_t
-            e_t = e_pool.tile([P, S + 32], BF16, tag="e")
+            e_t = e_pool.tile([P, S], BF16, tag="e")
+            for half in range(2):
+                nc.scalar.activation(
+                    out=e_t[:, 512 * half : 512 * half + 512],
+                    in_=sc[i][half][:],
+                    func=ACT.Exp,
+                    bias=negm[i][:],
+                    scale=SCALE,
+                    accum_out=den[i // 4][:, j, half : half + 1],
+                )
             nc.scalar.activation(
-                out=e_t[:, 0 : S + 1],
-                in_=s_bufs[j][:, 0 : S + 1],
-                func=ACT.Exp,
-                bias=negm[i][:],
-                scale=1.0,
-                accum_out=den[i // 4][:, j : j + 1],
+                out=den[i // 4][:, j, 2:3], in_=sink32[:, h : h + 1], func=ACT.Exp, bias=negm[i][:], scale=1.0
             )
             e_sb[i] = e_t
 
@@ -184,7 +213,11 @@ def tile_deepseekv4attention_kernel(tc, query, key, value, attention_mask, sinks
 
         def p4(i):
             et_t = et_pool.tile([P, 2, P, 4], BF16, tag="et", align_bytes=64)
-            nc.scalar.copy(out=et_t[:], in_=tr_ps[i][:].rearrange("p (c t) q -> p c q t", t=4))
+            src = tr_ps[i][:].rearrange("p (c t) q -> p c q t", t=4)
+            if i % 2 == 0:
+                nc.scalar.copy(out=et_t[:], in_=src)
+            else:
+                nc.vector.tensor_copy(out=et_t[:], in_=src)
             et_sb[i] = et_t
 
         def p5(i):
@@ -218,8 +251,10 @@ def tile_deepseekv4attention_kernel(tc, query, key, value, attention_mask, sinks
             pv[quad] = pv_t
 
         def recip(quad):
+            d_t = small.tile([P, 4], F32, tag="dsum")
+            nc.vector.tensor_reduce(out=d_t[:], in_=den[quad][:], axis=AX.X, op=ALU.add)
             r_t = small.tile([P, 4], F32, tag="rden")
-            nc.vector.reciprocal(out=r_t[:], in_=den[quad][:])
+            nc.vector.reciprocal(out=r_t[:], in_=d_t[:])
             rden[quad] = r_t
 
         def p6(quad):
@@ -231,36 +266,44 @@ def tile_deepseekv4attention_kernel(tc, query, key, value, attention_mask, sinks
                 )
             nc.sync.dma_start(out=o_v[:, t, 4 * hq : 4 * hq + 4, :], in_=o_t[:])
 
+        nc.vector.tensor_copy(out=sink32[:], in_=sink_bf[:])
+        nc.vector.tensor_scalar(out=sinkc[:], in0=sink_bf[:], scalar1=RSCALE, scalar2=None, op0=ALU.mult)
         prep_kt(0)
         prep_qt_pe(0)
         prep_qt_copy(0)
+        prep_mask_pe(0)
+        prep_mask_copy(0)
         prep_v(0)
 
-        for i in range(-1, NU + 4):
-            quad_due = i - 3 >= 0 and (i - 3) % 4 == 3
-            quad = (i - 3) // 4
+        for i in range(-1, NU + 5):
+            quad_due = i - 4 >= 0 and (i - 4) % 4 == 3
+            quad = (i - 4) // 4
             prep_b = (i + 3) // 8 if (i + 3) % 8 == 0 and 0 < (i + 3) // 8 < NU // 8 else None
-            if i + 1 < NU:
-                qk(i + 1)
-            if quad_due:
-                recip(quad)
-            if 0 <= i < NU:
-                p1p2(i)
+            prep_m = i // 4 + 1 if i >= 0 and i % 4 == 0 and i // 4 + 1 < NT else None
             if 0 <= i - 1 < NU:
                 p3(i - 1)
+            if i + 1 < NU:
+                qk(i + 1)
+            if 0 <= i < NU:
+                p1p2(i)
             if quad_due:
+                recip(quad)
                 mx(quad)
             if 0 <= i - 1 < NU:
                 tr(i - 1)
             if prep_b is not None:
                 prep_qt_pe(prep_b)
+            if 0 <= i - 3 < NU:
+                p5(i - 3)
             if 0 <= i - 2 < NU:
                 p4(i - 2)
-                p5(i - 2)
             if quad_due:
                 p6(quad)
             if prep_b is not None:
                 prep_qt_copy(prep_b)
+            if prep_m is not None:
+                prep_mask_pe(prep_m)
+                prep_mask_copy(prep_m)
             if i == 40:
                 prep_kt(1)
                 prep_v(1)

@@ -20,7 +20,6 @@ D = 128
 NT = S // P
 NU = H * NT
 SCALE = 1.0 / (D ** 0.5)
-RSCALE = D ** 0.5
 FLOPS = 2 * 2 * H * S * S * D
 
 
@@ -30,7 +29,7 @@ def tile_deepseekv4attention_kernel(tc, query, key, value, attention_mask, sinks
         const = ctx.enter_context(tc.tile_pool(name="const", bufs=1))
         qt_pool = ctx.enter_context(tc.tile_pool(name="qtp", bufs=3))
         e_pool = ctx.enter_context(tc.tile_pool(name="ep", bufs=3))
-        et_pool = ctx.enter_context(tc.tile_pool(name="etp", bufs=3))
+        et_pool = ctx.enter_context(tc.tile_pool(name="etp", bufs=4))
         c_pool = ctx.enter_context(tc.tile_pool(name="cp", bufs=10))
         small = ctx.enter_context(tc.tile_pool(name="small", bufs=4))
         o_pool = ctx.enter_context(tc.tile_pool(name="op", bufs=3))
@@ -55,13 +54,9 @@ def tile_deepseekv4attention_kernel(tc, query, key, value, attention_mask, sinks
         v_codes = const.tile([P, HKV, 2 * D], U32, align_bytes=64)
         v_scales = const.tile([P, HKV, 2 * D], U8, align_bytes=64)
         ident = const.tile([P, P], BF16)
-        ident32 = const.tile([P, P], F32)
-        mask_t = const.tile([P, NT, NT, P], F32)
-        sink32 = const.tile([P, H], F32)
-        sinkc = const.tile([P, H], F32)
+        s_bufs = [const.tile([P, S + 8], F32, name="s_buf%d" % j) for j in range(4)]
 
         make_identity(nc, ident[:])
-        make_identity(nc, ident32[:])
 
         nc.scalar.dma_start(out=sink_bf[:], in_=sinks.partition_broadcast(P))
         nc.sync.dma_start(out=k_raw[:, 0], in_=k_v[:, 0])
@@ -79,11 +74,16 @@ def tile_deepseekv4attention_kernel(tc, query, key, value, attention_mask, sinks
         for h in range(8, H):
             nc.sync.dma_start(out=q_raw[:, h], in_=q_v[:, h])
 
-        def prep_kt(g):
+        kt_psum = {}
+
+        def prep_kt_pe(g):
             kt_ps = ps_q.tile([P, NT, P], BF16, tag="qt")
             for a in range(NT):
                 nc.tensor.transpose(out=kt_ps[:, a, :], in_=k_raw[:, g, a, :], identity=ident[:])
-            nc.scalar.copy(out=kt_sb[:, g, :], in_=kt_ps[:].rearrange("p a k -> p (a k)"))
+            kt_psum[g] = kt_ps
+
+        def prep_kt_copy(g):
+            nc.scalar.copy(out=kt_sb[:, g, :], in_=kt_psum[g][:].rearrange("p a k -> p (a k)"))
 
         def prep_v(g):
             vg = et_pool.tile([P, 2, D, 4], BF16, tag="vg", align_bytes=64)
@@ -96,16 +96,6 @@ def tile_deepseekv4attention_kernel(tc, query, key, value, attention_mask, sinks
 
         qt_sb = {}
         qt_ps = {}
-        m_ps = {}
-
-        def prep_mask_pe(t):
-            mp = ps_q.tile([P, NT, P], BF16, tag="qt")
-            for a in range(NT):
-                nc.tensor.transpose(out=mp[:, a, :], in_=mask_sb[:, t, P * a : P * a + P], identity=ident[:])
-            m_ps[t] = mp
-
-        def prep_mask_copy(t):
-            nc.scalar.activation(out=mask_t[:, t], in_=m_ps[t][:], func=ACT.Copy, scale=RSCALE)
 
         def prep_qt_pe(b):
             hq, tp = divmod(b, 4)
@@ -151,57 +141,43 @@ def tile_deepseekv4attention_kernel(tc, query, key, value, attention_mask, sinks
                     lhsT=qt_sb[i // 8][:, i % 8, :],
                     rhs=kt_sb[:, g, 512 * half : 512 * half + 512],
                     start=True,
-                    stop=False,
+                    stop=True,
                 )
-                for a4 in range(4):
-                    nc.tensor.matmul(
-                        out=sc_t[:, P * a4 : P * a4 + P],
-                        lhsT=mask_t[:, t, 4 * half + a4, :],
-                        rhs=ident32[:],
-                        is_transpose=True,
-                        start=False,
-                        stop=(a4 == 3),
-                    )
                 halves.append(sc_t)
             sc[i] = halves
 
         def p1p2(i):
             hq, t, j = where(i)
-            h = 4 * hq + j
-            mx2 = small.tile([P, 2], F32, tag="mx2")
+            s_t = s_bufs[j]
+            if t == 0:
+                nc.vector.tensor_copy(out=s_t[:, S : S + 1], in_=sink_bf[:, 4 * hq + j : 4 * hq + j + 1])
             for half in range(2):
-                nc.vector.tensor_reduce(out=mx2[:, half : half + 1], in_=sc[i][half][:], axis=AX.X, op=ALU.max)
-            mxx = small.tile([P, 1], F32, tag="mxx")
-            nc.vector.scalar_tensor_tensor(
-                out=mxx[:],
-                in0=mx2[:, 0:1],
-                scalar=mx2[:, 1:2],
-                in1=sinkc[:, h : h + 1],
-                op0=ALU.max,
-                op1=ALU.max,
-            )
+                cols = slice(512 * half, 512 * half + 512)
+                nc.vector.scalar_tensor_tensor(
+                    out=s_t[:, cols],
+                    in0=sc[i][half][:],
+                    scalar=SCALE,
+                    in1=mask_sb[:, t, cols],
+                    op0=ALU.mult,
+                    op1=ALU.add,
+                )
             nm = small.tile([P, 1], F32, tag="negm")
-            nc.vector.tensor_scalar(out=nm[:], in0=mxx[:], scalar1=-SCALE, scalar2=None, op0=ALU.mult)
+            nc.vector.tensor_reduce(out=nm[:], in_=s_t[:, 0 : S + 1], axis=AX.X, op=ALU.max, negate=True)
             negm[i] = nm
 
         def p3(i):
             hq, t, j = where(i)
-            h = 4 * hq + j
             if j == 0:
-                den_t = small.tile([P, 4, 3], F32, tag="den")
+                den_t = small.tile([P, 4], F32, tag="den")
                 den[i // 4] = den_t
-            e_t = e_pool.tile([P, S], BF16, tag="e")
-            for half in range(2):
-                nc.scalar.activation(
-                    out=e_t[:, 512 * half : 512 * half + 512],
-                    in_=sc[i][half][:],
-                    func=ACT.Exp,
-                    bias=negm[i][:],
-                    scale=SCALE,
-                    accum_out=den[i // 4][:, j, half : half + 1],
-                )
+            e_t = e_pool.tile([P, S + 32], BF16, tag="e")
             nc.scalar.activation(
-                out=den[i // 4][:, j, 2:3], in_=sink32[:, h : h + 1], func=ACT.Exp, bias=negm[i][:], scale=1.0
+                out=e_t[:, 0 : S + 1],
+                in_=s_bufs[j][:, 0 : S + 1],
+                func=ACT.Exp,
+                bias=negm[i][:],
+                scale=1.0,
+                accum_out=den[i // 4][:, j : j + 1],
             )
             e_sb[i] = e_t
 
@@ -213,11 +189,7 @@ def tile_deepseekv4attention_kernel(tc, query, key, value, attention_mask, sinks
 
         def p4(i):
             et_t = et_pool.tile([P, 2, P, 4], BF16, tag="et", align_bytes=64)
-            src = tr_ps[i][:].rearrange("p (c t) q -> p c q t", t=4)
-            if i % 2 == 0:
-                nc.scalar.copy(out=et_t[:], in_=src)
-            else:
-                nc.vector.tensor_copy(out=et_t[:], in_=src)
+            nc.scalar.copy(out=et_t[:], in_=tr_ps[i][:].rearrange("p (c t) q -> p c q t", t=4))
             et_sb[i] = et_t
 
         def p5(i):
@@ -251,10 +223,8 @@ def tile_deepseekv4attention_kernel(tc, query, key, value, attention_mask, sinks
             pv[quad] = pv_t
 
         def recip(quad):
-            d_t = small.tile([P, 4], F32, tag="dsum")
-            nc.vector.tensor_reduce(out=d_t[:], in_=den[quad][:], axis=AX.X, op=ALU.add)
             r_t = small.tile([P, 4], F32, tag="rden")
-            nc.vector.reciprocal(out=r_t[:], in_=d_t[:])
+            nc.vector.reciprocal(out=r_t[:], in_=den[quad][:])
             rden[quad] = r_t
 
         def p6(quad):
@@ -266,44 +236,45 @@ def tile_deepseekv4attention_kernel(tc, query, key, value, attention_mask, sinks
                 )
             nc.sync.dma_start(out=o_v[:, t, 4 * hq : 4 * hq + 4, :], in_=o_t[:])
 
-        nc.vector.tensor_copy(out=sink32[:], in_=sink_bf[:])
-        nc.vector.tensor_scalar(out=sinkc[:], in0=sink_bf[:], scalar1=RSCALE, scalar2=None, op0=ALU.mult)
-        prep_kt(0)
+        prep_kt_pe(0)
+        prep_kt_copy(0)
         prep_qt_pe(0)
         prep_qt_copy(0)
-        prep_mask_pe(0)
-        prep_mask_copy(0)
         prep_v(0)
 
-        for i in range(-1, NU + 5):
-            quad_due = i - 4 >= 0 and (i - 4) % 4 == 3
-            quad = (i - 4) // 4
-            prep_b = (i + 3) // 8 if (i + 3) % 8 == 0 and 0 < (i + 3) // 8 < NU // 8 else None
-            prep_m = i // 4 + 1 if i >= 0 and i % 4 == 0 and i // 4 + 1 < NT else None
+        def quad_at(i, lag):
+            last = i - lag
+            if 0 <= last < NU and last % 4 == 3:
+                return last // 4
+            return None
+
+        for i in range(-1, NU + 7):
+            q_mx = quad_at(i, 5)
+            q_out = quad_at(i, 6)
             if 0 <= i - 1 < NU:
                 p3(i - 1)
             if i + 1 < NU:
                 qk(i + 1)
+            if 0 <= i - 2 < NU:
+                tr(i - 2)
+            if q_mx is not None:
+                recip(q_mx)
             if 0 <= i < NU:
                 p1p2(i)
-            if quad_due:
-                recip(quad)
-                mx(quad)
-            if 0 <= i - 1 < NU:
-                tr(i - 1)
-            if prep_b is not None:
-                prep_qt_pe(prep_b)
+            if 0 <= i - 4 < NU:
+                p5(i - 4)
+            if q_mx is not None:
+                mx(q_mx)
             if 0 <= i - 3 < NU:
-                p5(i - 3)
-            if 0 <= i - 2 < NU:
-                p4(i - 2)
-            if quad_due:
-                p6(quad)
-            if prep_b is not None:
-                prep_qt_copy(prep_b)
-            if prep_m is not None:
-                prep_mask_pe(prep_m)
-                prep_mask_copy(prep_m)
-            if i == 40:
-                prep_kt(1)
+                p4(i - 3)
+            if q_out is not None:
+                p6(q_out)
+            if (i + 5) % 8 == 0 and 0 < (i + 5) // 8 < NU // 8:
+                prep_qt_pe((i + 5) // 8)
+            if (i + 4) % 8 == 0 and 0 < (i + 4) // 8 < NU // 8:
+                prep_qt_copy((i + 4) // 8)
+            if i == 41:
+                prep_kt_pe(1)
                 prep_v(1)
+            if i == 42:
+                prep_kt_copy(1)

@@ -20,6 +20,7 @@ D = 128
 NT = S // P
 NU = H * NT
 SCALE = 1.0 / (D ** 0.5)
+RSCALE = D ** 0.5
 FLOPS = 2 * 2 * H * S * S * D
 
 
@@ -33,11 +34,10 @@ def tile_deepseekv4attention_kernel(tc, query, key, value, attention_mask, sinks
         c_pool = ctx.enter_context(tc.tile_pool(name="cp", bufs=10))
         small = ctx.enter_context(tc.tile_pool(name="small", bufs=4))
         o_pool = ctx.enter_context(tc.tile_pool(name="op", bufs=3))
-        ps_s = ctx.enter_context(tc.psum_pool(name="ps_s", bufs=4))
+        ps_a = ctx.enter_context(tc.psum_pool(name="ps_a", bufs=2))
+        ps_c = ctx.enter_context(tc.psum_pool(name="ps_c", bufs=3))
         ps_t = ctx.enter_context(tc.psum_pool(name="ps_t", bufs=2))
-        ps_o = ctx.enter_context(tc.psum_pool(name="ps_o", bufs=1))
-        ps_q = ctx.enter_context(tc.psum_pool(name="ps_q", bufs=1))
-        ctx.enter_context(tc.manual_schedule())
+        ps_x = ctx.enter_context(tc.psum_pool(name="ps_x", bufs=1))
 
         q_v = query[0].rearrange("h (p t) d -> p h t d", t=NT)
         m_v = attention_mask[0, 0].rearrange("(p t) k -> p t k", t=NT)
@@ -47,16 +47,21 @@ def tile_deepseekv4attention_kernel(tc, query, key, value, attention_mask, sinks
 
         q_raw = const.tile([P, H, NT, D], BF16)
         mask_sb = const.tile([P, NT, S], BF16)
+        mask_t = const.tile([P, NT, NT, P], F32)
         k_raw = const.tile([P, HKV, NT, D], BF16)
         v_raw = const.tile([P, HKV, NT, D], BF16)
         sink_bf = const.tile([P, H], BF16)
+        sink32 = const.tile([P, H], F32)
+        sinkc = const.tile([P, H], F32)
         kt_sb = const.tile([P, HKV, S], BF16)
         v_codes = const.tile([P, HKV, 2 * D], U32, align_bytes=64)
         v_scales = const.tile([P, HKV, 2 * D], U8, align_bytes=64)
         ident = const.tile([P, P], BF16)
+        ident32 = const.tile([P, P], F32)
         s_bufs = [const.tile([P, S + 8], F32, name="s_buf%d" % j) for j in range(4)]
 
         make_identity(nc, ident[:])
+        make_identity(nc, ident32[:])
 
         nc.scalar.dma_start(out=sink_bf[:], in_=sinks.partition_broadcast(P))
         nc.sync.dma_start(out=k_raw[:, 0], in_=k_v[:, 0])
@@ -74,16 +79,20 @@ def tile_deepseekv4attention_kernel(tc, query, key, value, attention_mask, sinks
         for h in range(8, H):
             nc.sync.dma_start(out=q_raw[:, h], in_=q_v[:, h])
 
-        kt_psum = {}
+        def in_psum(i):
+            return i % 2 == 1
 
-        def prep_kt_pe(g):
-            kt_ps = ps_q.tile([P, NT, P], BF16, tag="qt")
+        def prep_kt(g):
+            kt_ps = ps_x.tile([P, NT, P], BF16, tag="x")
             for a in range(NT):
                 nc.tensor.transpose(out=kt_ps[:, a, :], in_=k_raw[:, g, a, :], identity=ident[:])
-            kt_psum[g] = kt_ps
+            nc.scalar.copy(out=kt_sb[:, g, :], in_=kt_ps[:].rearrange("p a k -> p (a k)"))
 
-        def prep_kt_copy(g):
-            nc.scalar.copy(out=kt_sb[:, g, :], in_=kt_psum[g][:].rearrange("p a k -> p (a k)"))
+        def prep_mask(t):
+            mp = ps_x.tile([P, NT, P], BF16, tag="x")
+            for a in range(NT):
+                nc.tensor.transpose(out=mp[:, a, :], in_=mask_sb[:, t, P * a : P * a + P], identity=ident[:])
+            nc.scalar.activation(out=mask_t[:, t], in_=mp[:], func=ACT.Copy, scale=RSCALE)
 
         def prep_v(g):
             vg = et_pool.tile([P, 2, D, 4], BF16, tag="vg", align_bytes=64)
@@ -95,11 +104,10 @@ def tile_deepseekv4attention_kernel(tc, query, key, value, attention_mask, sinks
             )
 
         qt_sb = {}
-        qt_ps = {}
 
-        def prep_qt_pe(b):
+        def prep_qt(b):
             hq, tp = divmod(b, 4)
-            q_ps = ps_q.tile([P, 8, P], BF16, tag="qt")
+            q_ps = ps_x.tile([P, 8, P], BF16, tag="x")
             for t2 in range(2):
                 for j in range(4):
                     nc.tensor.transpose(
@@ -107,14 +115,12 @@ def tile_deepseekv4attention_kernel(tc, query, key, value, attention_mask, sinks
                         in_=q_raw[:, 4 * hq + j, 2 * tp + t2, :],
                         identity=ident[:],
                     )
-            qt_ps[b] = q_ps
-
-        def prep_qt_copy(b):
             qt = qt_pool.tile([P, 8, P], BF16, tag="qtsb")
-            nc.scalar.copy(out=qt[:], in_=qt_ps[b][:])
+            nc.vector.tensor_copy(out=qt[:], in_=q_ps[:])
             qt_sb[b] = qt
 
         sc = {}
+        mx2s = {}
         negm = {}
         den = {}
         rden = {}
@@ -130,27 +136,51 @@ def tile_deepseekv4attention_kernel(tc, query, key, value, attention_mask, sinks
             t, j = divmod(r, 4)
             return hq, t, j
 
+        def s_of(i):
+            hq, t, j = where(i)
+            return s_bufs[(j // 2) * 2 + t % 2]
+
         def qk(i):
             hq, t, j = where(i)
             g = (4 * hq + j) // (H // HKV)
             halves = []
             for half in range(2):
-                sc_t = ps_s.tile([P, 512], F32, tag="sc", name="sc_t")
+                if in_psum(i):
+                    sc_t = ps_c.tile([P, 512], F32, tag="scc", name="sc_c")
+                else:
+                    sc_t = ps_a.tile([P, 512], F32, tag="sca", name="sc_a")
                 nc.tensor.matmul(
                     out=sc_t[:],
                     lhsT=qt_sb[i // 8][:, i % 8, :],
                     rhs=kt_sb[:, g, 512 * half : 512 * half + 512],
                     start=True,
-                    stop=True,
+                    stop=not in_psum(i),
                 )
+                if in_psum(i):
+                    for a4 in range(4):
+                        nc.tensor.matmul(
+                            out=sc_t[:, P * a4 : P * a4 + P],
+                            lhsT=mask_t[:, t, 4 * half + a4, :],
+                            rhs=ident32[:],
+                            is_transpose=True,
+                            start=False,
+                            stop=(a4 == 3),
+                        )
                 halves.append(sc_t)
             sc[i] = halves
 
-        def p1p2(i):
+        def p1(i):
             hq, t, j = where(i)
-            s_t = s_bufs[j]
-            if t == 0:
-                nc.vector.tensor_copy(out=s_t[:, S : S + 1], in_=sink_bf[:, 4 * hq + j : 4 * hq + j + 1])
+            h = 4 * hq + j
+            if in_psum(i):
+                mx2 = small.tile([P, 2], F32, tag="mx2")
+                for half in range(2):
+                    nc.vector.tensor_reduce(out=mx2[:, half : half + 1], in_=sc[i][half][:], axis=AX.X, op=ALU.max)
+                mx2s[i] = mx2
+                return
+            s_t = s_of(i)
+            if t < 2:
+                nc.vector.tensor_copy(out=s_t[:, S : S + 1], in_=sink_bf[:, h : h + 1])
             for half in range(2):
                 cols = slice(512 * half, 512 * half + 512)
                 nc.vector.scalar_tensor_tensor(
@@ -161,24 +191,57 @@ def tile_deepseekv4attention_kernel(tc, query, key, value, attention_mask, sinks
                     op0=ALU.mult,
                     op1=ALU.add,
                 )
+
+        def p2(i):
+            hq, t, j = where(i)
+            h = 4 * hq + j
             nm = small.tile([P, 1], F32, tag="negm")
-            nc.vector.tensor_reduce(out=nm[:], in_=s_t[:, 0 : S + 1], axis=AX.X, op=ALU.max, negate=True)
+            if in_psum(i):
+                mxx = small.tile([P, 1], F32, tag="mxx")
+                nc.vector.scalar_tensor_tensor(
+                    out=mxx[:],
+                    in0=mx2s[i][:, 0:1],
+                    scalar=mx2s[i][:, 1:2],
+                    in1=sinkc[:, h : h + 1],
+                    op0=ALU.max,
+                    op1=ALU.max,
+                )
+                nc.vector.tensor_scalar(out=nm[:], in0=mxx[:], scalar1=-SCALE, scalar2=None, op0=ALU.mult)
+            else:
+                nc.vector.tensor_reduce(out=nm[:], in_=s_of(i)[:, 0 : S + 1], axis=AX.X, op=ALU.max, negate=True)
             negm[i] = nm
 
         def p3(i):
             hq, t, j = where(i)
+            h = 4 * hq + j
             if j == 0:
-                den_t = small.tile([P, 4], F32, tag="den")
+                den_t = small.tile([P, 4, 3], F32, tag="den")
+                nc.gpsimd.memset(den_t[:], 0.0)
                 den[i // 4] = den_t
+            den_t = den[i // 4]
             e_t = e_pool.tile([P, S + 32], BF16, tag="e")
-            nc.scalar.activation(
-                out=e_t[:, 0 : S + 1],
-                in_=s_bufs[j][:, 0 : S + 1],
-                func=ACT.Exp,
-                bias=negm[i][:],
-                scale=1.0,
-                accum_out=den[i // 4][:, j : j + 1],
-            )
+            if in_psum(i):
+                for half in range(2):
+                    nc.scalar.activation(
+                        out=e_t[:, 512 * half : 512 * half + 512],
+                        in_=sc[i][half][:],
+                        func=ACT.Exp,
+                        bias=negm[i][:],
+                        scale=SCALE,
+                        accum_out=den_t[:, j, half : half + 1],
+                    )
+                nc.scalar.activation(
+                    out=den_t[:, j, 2:3], in_=sink32[:, h : h + 1], func=ACT.Exp, bias=negm[i][:], scale=1.0
+                )
+            else:
+                nc.scalar.activation(
+                    out=e_t[:, 0 : S + 1],
+                    in_=s_of(i)[:, 0 : S + 1],
+                    func=ACT.Exp,
+                    bias=negm[i][:],
+                    scale=1.0,
+                    accum_out=den_t[:, j, 0:1],
+                )
             e_sb[i] = e_t
 
         def tr(i):
@@ -189,7 +252,11 @@ def tile_deepseekv4attention_kernel(tc, query, key, value, attention_mask, sinks
 
         def p4(i):
             et_t = et_pool.tile([P, 2, P, 4], BF16, tag="et", align_bytes=64)
-            nc.scalar.copy(out=et_t[:], in_=tr_ps[i][:].rearrange("p (c t) q -> p c q t", t=4))
+            src = tr_ps[i][:].rearrange("p (c t) q -> p c q t", t=4)
+            if i % 4 == 3:
+                nc.vector.tensor_copy(out=et_t[:], in_=src)
+            else:
+                nc.scalar.copy(out=et_t[:], in_=src)
             et_sb[i] = et_t
 
         def p5(i):
@@ -204,7 +271,7 @@ def tile_deepseekv4attention_kernel(tc, query, key, value, attention_mask, sinks
             scales[i] = sc_b
 
         def mx(quad):
-            pv_t = ps_o.tile([P, 4, D], F32, tag="pv")
+            pv_t = ps_x.tile([P, 4, D], F32, tag="x")
             for j in range(4):
                 i = 4 * quad + j
                 hq = where(i)[0]
@@ -223,8 +290,10 @@ def tile_deepseekv4attention_kernel(tc, query, key, value, attention_mask, sinks
             pv[quad] = pv_t
 
         def recip(quad):
+            d_t = small.tile([P, 4], F32, tag="dsum")
+            nc.vector.tensor_reduce(out=d_t[:], in_=den[quad][:], axis=AX.X, op=ALU.add)
             r_t = small.tile([P, 4], F32, tag="rden")
-            nc.vector.reciprocal(out=r_t[:], in_=den[quad][:])
+            nc.vector.reciprocal(out=r_t[:], in_=d_t[:])
             rden[quad] = r_t
 
         def p6(quad):
@@ -236,10 +305,11 @@ def tile_deepseekv4attention_kernel(tc, query, key, value, attention_mask, sinks
                 )
             nc.sync.dma_start(out=o_v[:, t, 4 * hq : 4 * hq + 4, :], in_=o_t[:])
 
-        prep_kt_pe(0)
-        prep_kt_copy(0)
-        prep_qt_pe(0)
-        prep_qt_copy(0)
+        nc.vector.tensor_copy(out=sink32[:], in_=sink_bf[:])
+        nc.vector.tensor_scalar(out=sinkc[:], in0=sink_bf[:], scalar1=RSCALE, scalar2=None, op0=ALU.mult)
+        prep_kt(0)
+        prep_qt(0)
+        prep_mask(0)
         prep_v(0)
 
         def quad_at(i, lag):
@@ -248,33 +318,33 @@ def tile_deepseekv4attention_kernel(tc, query, key, value, attention_mask, sinks
                 return last // 4
             return None
 
-        for i in range(-1, NU + 7):
-            q_mx = quad_at(i, 5)
-            q_out = quad_at(i, 6)
-            if 0 <= i - 1 < NU:
-                p3(i - 1)
+        for i in range(-1, NU + 8):
+            q_mx = quad_at(i, 6)
+            q_out = quad_at(i, 7)
+            if 0 <= i - 2 < NU:
+                p3(i - 2)
             if i + 1 < NU:
                 qk(i + 1)
-            if 0 <= i - 2 < NU:
-                tr(i - 2)
+            if 0 <= i - 3 < NU:
+                tr(i - 3)
             if q_mx is not None:
                 recip(q_mx)
             if 0 <= i < NU:
-                p1p2(i)
-            if 0 <= i - 4 < NU:
-                p5(i - 4)
+                p1(i)
+            if 0 <= i - 1 < NU:
+                p2(i - 1)
+            if 0 <= i - 5 < NU:
+                p5(i - 5)
             if q_mx is not None:
                 mx(q_mx)
-            if 0 <= i - 3 < NU:
-                p4(i - 3)
+            if 0 <= i - 4 < NU:
+                p4(i - 4)
             if q_out is not None:
                 p6(q_out)
             if (i + 5) % 8 == 0 and 0 < (i + 5) // 8 < NU // 8:
-                prep_qt_pe((i + 5) // 8)
-            if (i + 4) % 8 == 0 and 0 < (i + 4) // 8 < NU // 8:
-                prep_qt_copy((i + 4) // 8)
+                prep_qt((i + 5) // 8)
+            if i >= 0 and i % 4 == 0 and i // 4 + 1 < NT:
+                prep_mask(i // 4 + 1)
             if i == 41:
-                prep_kt_pe(1)
+                prep_kt(1)
                 prep_v(1)
-            if i == 42:
-                prep_kt_copy(1)

@@ -17,8 +17,11 @@ H = 16
 HKV = 2
 S = 1024
 D = 128
+HALF = S // 2
 NT = S // P
 NU = H * NT
+NQ = NU // 4
+PAD = 8
 SCALE = 1.0 / (D ** 0.5)
 RSCALE = D ** 0.5
 FLOPS = 2 * 2 * H * S * S * D
@@ -30,14 +33,16 @@ def tile_deepseekv4attention_kernel(tc, query, key, value, attention_mask, sinks
         const = ctx.enter_context(tc.tile_pool(name="const", bufs=1))
         qt_pool = ctx.enter_context(tc.tile_pool(name="qtp", bufs=3))
         e_pool = ctx.enter_context(tc.tile_pool(name="ep", bufs=3))
-        et_pool = ctx.enter_context(tc.tile_pool(name="etp", bufs=4))
-        c_pool = ctx.enter_context(tc.tile_pool(name="cp", bufs=10))
+        pl_pool = ctx.enter_context(tc.tile_pool(name="plp", bufs=3))
+        et_pool = ctx.enter_context(tc.tile_pool(name="etp", bufs=1))
+        c_pool = ctx.enter_context(tc.tile_pool(name="cp", bufs=2))
         small = ctx.enter_context(tc.tile_pool(name="small", bufs=4))
         o_pool = ctx.enter_context(tc.tile_pool(name="op", bufs=3))
         ps_a = ctx.enter_context(tc.psum_pool(name="ps_a", bufs=2))
         ps_c = ctx.enter_context(tc.psum_pool(name="ps_c", bufs=3))
         ps_t = ctx.enter_context(tc.psum_pool(name="ps_t", bufs=2))
         ps_x = ctx.enter_context(tc.psum_pool(name="ps_x", bufs=1))
+        ctx.enter_context(tc.manual_schedule())
 
         q_v = query[0].rearrange("h (p t) d -> p h t d", t=NT)
         m_v = attention_mask[0, 0].rearrange("(p t) k -> p t k", t=NT)
@@ -47,18 +52,17 @@ def tile_deepseekv4attention_kernel(tc, query, key, value, attention_mask, sinks
 
         q_raw = const.tile([P, H, NT, D], BF16)
         mask_sb = const.tile([P, NT, S], BF16)
-        mask_t = const.tile([P, NT, NT, P], F32)
+        mask_t = const.tile([P, NT, 4, P], F32)
         k_raw = const.tile([P, HKV, NT, D], BF16)
         v_raw = const.tile([P, HKV, NT, D], BF16)
         sink_bf = const.tile([P, H], BF16)
-        sink32 = const.tile([P, H], F32)
-        sinkc = const.tile([P, H], F32)
         kt_sb = const.tile([P, HKV, S], BF16)
         v_codes = const.tile([P, HKV, 2 * D], U32, align_bytes=64)
         v_scales = const.tile([P, HKV, 2 * D], U8, align_bytes=64)
+        v_grouped = const.tile([P, 2, D, 4], BF16, align_bytes=64)
         ident = const.tile([P, P], BF16)
         ident32 = const.tile([P, P], F32)
-        s_bufs = [const.tile([P, S + 8], F32, name="s_buf%d" % j) for j in range(4)]
+        s_bufs = [const.tile([P, PAD + HALF], F32, name="s_buf%d" % j) for j in range(4)]
 
         make_identity(nc, ident[:])
         make_identity(nc, ident32[:])
@@ -67,9 +71,8 @@ def tile_deepseekv4attention_kernel(tc, query, key, value, attention_mask, sinks
         nc.sync.dma_start(out=k_raw[:, 0], in_=k_v[:, 0])
         for h in range(4):
             nc.sync.dma_start(out=q_raw[:, h], in_=q_v[:, h])
-        nc.sync.dma_start(out=mask_sb[:, 0, :], in_=m_v[:, 0, :])
+        nc.sync.dma_start(out=mask_sb[:, 0:2, :], in_=m_v[:, 0:2, :])
         nc.sync.dma_start(out=v_raw[:, 0], in_=v_v[:, 0])
-        nc.sync.dma_start(out=mask_sb[:, 1, :], in_=m_v[:, 1, :])
         nc.sync.dma_start(out=mask_sb[:, 2:4, :], in_=m_v[:, 2:4, :])
         nc.sync.dma_start(out=mask_sb[:, 4:8, :], in_=m_v[:, 4:8, :])
         for h in range(4, 8):
@@ -79,33 +82,44 @@ def tile_deepseekv4attention_kernel(tc, query, key, value, attention_mask, sinks
         for h in range(8, H):
             nc.sync.dma_start(out=q_raw[:, h], in_=q_v[:, h])
 
-        def in_psum(i):
-            return i % 2 == 1
+        x_ps = {}
 
-        def prep_kt(g):
+        def prep_kt_pe(g):
             kt_ps = ps_x.tile([P, NT, P], BF16, tag="x")
             for a in range(NT):
                 nc.tensor.transpose(out=kt_ps[:, a, :], in_=k_raw[:, g, a, :], identity=ident[:])
-            nc.scalar.copy(out=kt_sb[:, g, :], in_=kt_ps[:].rearrange("p a k -> p (a k)"))
+            x_ps["k%d" % g] = kt_ps
 
-        def prep_mask(t):
-            mp = ps_x.tile([P, NT, P], BF16, tag="x")
-            for a in range(NT):
-                nc.tensor.transpose(out=mp[:, a, :], in_=mask_sb[:, t, P * a : P * a + P], identity=ident[:])
-            nc.scalar.activation(out=mask_t[:, t], in_=mp[:], func=ACT.Copy, scale=RSCALE)
+        def prep_kt_copy(g):
+            nc.scalar.copy(out=kt_sb[:, g, :], in_=x_ps["k%d" % g][:].rearrange("p a k -> p (a k)"))
+
+        def prep_mask_pe(tp):
+            mp = ps_x.tile([P, 2, 4, P], BF16, tag="x")
+            for t2 in range(2):
+                for a in range(4):
+                    nc.tensor.transpose(
+                        out=mp[:, t2, a, :],
+                        in_=mask_sb[:, 2 * tp + t2, HALF + P * a : HALF + P * a + P],
+                        identity=ident[:],
+                    )
+            x_ps["m%d" % tp] = mp
+
+        def prep_mask_copy(tp):
+            nc.scalar.activation(
+                out=mask_t[:, 2 * tp : 2 * tp + 2], in_=x_ps["m%d" % tp][:], func=ACT.Copy, scale=RSCALE
+            )
 
         def prep_v(g):
-            vg = et_pool.tile([P, 2, D, 4], BF16, tag="vg", align_bytes=64)
-            nc.vector.tensor_copy(out=vg[:], in_=v_raw[:, g].rearrange("p (c t) d -> p c d t", t=4))
+            nc.vector.tensor_copy(out=v_grouped[:], in_=v_raw[:, g].rearrange("p (c t) d -> p c d t", t=4))
             nc.vector.quantize_mx(
                 out=v_codes[:, g, :].bitcast(FP8X4),
                 scales=v_scales[:, g, :],
-                in_=vg[:].rearrange("p c d t -> p (c d t)"),
+                in_=v_grouped[:].rearrange("p c d t -> p (c d t)"),
             )
 
         qt_sb = {}
 
-        def prep_qt(b):
+        def prep_qt_pe(b):
             hq, tp = divmod(b, 4)
             q_ps = ps_x.tile([P, 8, P], BF16, tag="x")
             for t2 in range(2):
@@ -115,17 +129,24 @@ def tile_deepseekv4attention_kernel(tc, query, key, value, attention_mask, sinks
                         in_=q_raw[:, 4 * hq + j, 2 * tp + t2, :],
                         identity=ident[:],
                     )
+            x_ps["q%d" % b] = q_ps
+
+        def prep_qt_copy(b):
             qt = qt_pool.tile([P, 8, P], BF16, tag="qtsb")
-            nc.vector.tensor_copy(out=qt[:], in_=q_ps[:])
+            nc.scalar.copy(out=qt[:], in_=x_ps["q%d" % b][:])
             qt_sb[b] = qt
 
-        sc = {}
-        mx2s = {}
+        sc_a = {}
+        sc_c = {}
+        nm0 = {}
+        nm1 = {}
         negm = {}
         den = {}
+        dsum = {}
         rden = {}
         e_sb = {}
         tr_ps = {}
+        plain = {}
         et_sb = {}
         codes = {}
         scales = {}
@@ -136,164 +157,153 @@ def tile_deepseekv4attention_kernel(tc, query, key, value, attention_mask, sinks
             t, j = divmod(r, 4)
             return hq, t, j
 
-        def s_of(i):
-            hq, t, j = where(i)
-            return s_bufs[(j // 2) * 2 + t % 2]
-
         def qk(i):
             hq, t, j = where(i)
             g = (4 * hq + j) // (H // HKV)
-            halves = []
-            for half in range(2):
-                if in_psum(i):
-                    sc_t = ps_c.tile([P, 512], F32, tag="scc", name="sc_c")
-                else:
-                    sc_t = ps_a.tile([P, 512], F32, tag="sca", name="sc_a")
+            c_t = ps_c.tile([P, HALF], F32, tag="scc")
+            nc.tensor.matmul(
+                out=c_t[:], lhsT=qt_sb[i // 8][:, i % 8, :], rhs=kt_sb[:, g, HALF:S], start=True, stop=False
+            )
+            for a in range(4):
                 nc.tensor.matmul(
-                    out=sc_t[:],
-                    lhsT=qt_sb[i // 8][:, i % 8, :],
-                    rhs=kt_sb[:, g, 512 * half : 512 * half + 512],
-                    start=True,
-                    stop=not in_psum(i),
+                    out=c_t[:, P * a : P * a + P],
+                    lhsT=mask_t[:, t, a, :],
+                    rhs=ident32[:],
+                    is_transpose=True,
+                    start=False,
+                    stop=(a == 3),
                 )
-                if in_psum(i):
-                    for a4 in range(4):
-                        nc.tensor.matmul(
-                            out=sc_t[:, P * a4 : P * a4 + P],
-                            lhsT=mask_t[:, t, 4 * half + a4, :],
-                            rhs=ident32[:],
-                            is_transpose=True,
-                            start=False,
-                            stop=(a4 == 3),
-                        )
-                halves.append(sc_t)
-            sc[i] = halves
+            sc_c[i] = c_t
+            a_t = ps_a.tile([P, HALF], F32, tag="sca")
+            nc.tensor.matmul(
+                out=a_t[:], lhsT=qt_sb[i // 8][:, i % 8, :], rhs=kt_sb[:, g, 0:HALF], start=True, stop=True
+            )
+            sc_a[i] = a_t
 
-        def p1(i):
+        def stt(i):
             hq, t, j = where(i)
             h = 4 * hq + j
-            if in_psum(i):
-                mx2 = small.tile([P, 2], F32, tag="mx2")
-                for half in range(2):
-                    nc.vector.tensor_reduce(out=mx2[:, half : half + 1], in_=sc[i][half][:], axis=AX.X, op=ALU.max)
-                mx2s[i] = mx2
-                return
-            s_t = s_of(i)
-            if t < 2:
-                nc.vector.tensor_copy(out=s_t[:, S : S + 1], in_=sink_bf[:, h : h + 1])
-            for half in range(2):
-                cols = slice(512 * half, 512 * half + 512)
-                nc.vector.scalar_tensor_tensor(
-                    out=s_t[:, cols],
-                    in0=sc[i][half][:],
-                    scalar=SCALE,
-                    in1=mask_sb[:, t, cols],
-                    op0=ALU.mult,
-                    op1=ALU.add,
-                )
+            s_t = s_bufs[j]
+            if t == 0:
+                nc.vector.tensor_copy(out=s_t[:, PAD - 1 : PAD], in_=sink_bf[:, h : h + 1])
+            nc.vector.scalar_tensor_tensor(
+                out=s_t[:, PAD : PAD + HALF],
+                in0=sc_a[i][:],
+                scalar=SCALE,
+                in1=mask_sb[:, t, 0:HALF],
+                op0=ALU.mult,
+                op1=ALU.add,
+            )
 
-        def p2(i):
-            hq, t, j = where(i)
-            h = 4 * hq + j
-            nm = small.tile([P, 1], F32, tag="negm")
-            if in_psum(i):
-                mxx = small.tile([P, 1], F32, tag="mxx")
-                nc.vector.scalar_tensor_tensor(
-                    out=mxx[:],
-                    in0=mx2s[i][:, 0:1],
-                    scalar=mx2s[i][:, 1:2],
-                    in1=sinkc[:, h : h + 1],
-                    op0=ALU.max,
-                    op1=ALU.max,
-                )
-                nc.vector.tensor_scalar(out=nm[:], in0=mxx[:], scalar1=-SCALE, scalar2=None, op0=ALU.mult)
-            else:
-                nc.vector.tensor_reduce(out=nm[:], in_=s_of(i)[:, 0 : S + 1], axis=AX.X, op=ALU.max, negate=True)
-            negm[i] = nm
+        def r1(i):
+            n_t = small.tile([P, 1], F32, tag="nm1")
+            nc.vector.tensor_reduce(out=n_t[:], in_=sc_c[i][:], axis=AX.X, op=ALU.max, negate=True)
+            nm1[i] = n_t
 
-        def p3(i):
-            hq, t, j = where(i)
-            h = 4 * hq + j
+        def r0(i):
+            n_t = small.tile([P, 1], F32, tag="nm0")
+            nc.vector.tensor_reduce(
+                out=n_t[:], in_=s_bufs[i % 4][:, PAD - 1 : PAD + HALF], axis=AX.X, op=ALU.max, negate=True
+            )
+            nm0[i] = n_t
+
+        def tn(i):
+            n_t = small.tile([P, 1], F32, tag="negm")
+            nc.vector.tensor_scalar(
+                out=n_t[:], in0=nm1[i][:], scalar1=SCALE, scalar2=nm0[i][:], op0=ALU.mult, op1=ALU.min
+            )
+            negm[i] = n_t
+
+        def ex(i):
+            j = i % 4
             if j == 0:
-                den_t = small.tile([P, 4, 3], F32, tag="den")
-                nc.gpsimd.memset(den_t[:], 0.0)
+                den_t = small.tile([P, 4, 2], F32, tag="den")
                 den[i // 4] = den_t
             den_t = den[i // 4]
-            e_t = e_pool.tile([P, S + 32], BF16, tag="e")
-            if in_psum(i):
-                for half in range(2):
-                    nc.scalar.activation(
-                        out=e_t[:, 512 * half : 512 * half + 512],
-                        in_=sc[i][half][:],
-                        func=ACT.Exp,
-                        bias=negm[i][:],
-                        scale=SCALE,
-                        accum_out=den_t[:, j, half : half + 1],
-                    )
-                nc.scalar.activation(
-                    out=den_t[:, j, 2:3], in_=sink32[:, h : h + 1], func=ACT.Exp, bias=negm[i][:], scale=1.0
-                )
-            else:
-                nc.scalar.activation(
-                    out=e_t[:, 0 : S + 1],
-                    in_=s_of(i)[:, 0 : S + 1],
-                    func=ACT.Exp,
-                    bias=negm[i][:],
-                    scale=1.0,
-                    accum_out=den_t[:, j, 0:1],
-                )
+            e_t = e_pool.tile([P, PAD + S], BF16, tag="e")
+            nc.scalar.activation(
+                out=e_t[:, PAD + HALF : PAD + S],
+                in_=sc_c[i][:],
+                func=ACT.Exp,
+                bias=negm[i][:],
+                scale=SCALE,
+                accum_out=den_t[:, j, 1:2],
+            )
+            nc.scalar.activation(
+                out=e_t[:, PAD - 1 : PAD + HALF],
+                in_=s_bufs[j][:, PAD - 1 : PAD + HALF],
+                func=ACT.Exp,
+                bias=negm[i][:],
+                scale=1.0,
+                accum_out=den_t[:, j, 0:1],
+            )
             e_sb[i] = e_t
 
         def tr(i):
             tr_t = ps_t.tile([P, 8, P], BF16, tag="tr")
             for a in range(8):
-                nc.tensor.transpose(out=tr_t[:, a, :], in_=e_sb[i][:, P * a : P * a + P], identity=ident[:])
+                nc.tensor.transpose(
+                    out=tr_t[:, a, :], in_=e_sb[i][:, PAD + P * a : PAD + P * a + P], identity=ident[:]
+                )
             tr_ps[i] = tr_t
 
         def p4(i):
-            et_t = et_pool.tile([P, 2, P, 4], BF16, tag="et", align_bytes=64)
-            src = tr_ps[i][:].rearrange("p (c t) q -> p c q t", t=4)
-            if i % 4 == 3:
-                nc.vector.tensor_copy(out=et_t[:], in_=src)
-            else:
-                nc.scalar.copy(out=et_t[:], in_=src)
-            et_sb[i] = et_t
+            j = i % 4
+            if j == 0:
+                pl_t = pl_pool.tile([P, 4, S], BF16, tag="plain")
+                plain[i // 4] = pl_t
+            nc.scalar.copy(out=plain[i // 4][:, j, :], in_=tr_ps[i][:].rearrange("p a q -> p (a q)"))
 
-        def p5(i):
-            c_t = c_pool.tile([P, 2 * P], U32, tag="codes", align_bytes=64)
-            sc_b = c_pool.tile([P, 2 * P], U8, tag="scales", align_bytes=64)
+        def regroup(quad):
+            et_t = et_pool.tile([P, 8, P, 4], BF16, tag="et", align_bytes=64)
+            nc.gpsimd.tensor_scalar(
+                out=et_t[:],
+                in0=plain[quad][:].rearrange("p j (c t q) -> p (j c) q t", c=2, t=4),
+                scalar1=1.0,
+                scalar2=0.0,
+                op0=ALU.mult,
+                op1=ALU.add,
+            )
+            et_sb[quad] = et_t
+
+        def quantise(quad):
+            c_t = c_pool.tile([P, 8 * P], U32, tag="codes", align_bytes=64)
+            sc_b = c_pool.tile([P, 8 * P], U8, tag="scales", align_bytes=64)
             nc.vector.quantize_mx(
                 out=c_t[:].bitcast(FP8X4),
                 scales=sc_b[:],
-                in_=et_sb[i][:].rearrange("p c q t -> p (c q t)"),
+                in_=et_sb[quad][:].rearrange("p c q t -> p (c q t)"),
             )
-            codes[i] = c_t
-            scales[i] = sc_b
+            codes[quad] = c_t
+            scales[quad] = sc_b
 
         def mx(quad):
             pv_t = ps_x.tile([P, 4, D], F32, tag="x")
+            hq = where(4 * quad)[0]
             for j in range(4):
-                i = 4 * quad + j
-                hq = where(i)[0]
                 g = (4 * hq + j) // (H // HKV)
                 for c in range(2):
-                    cols = slice(P * c, P * c + P)
+                    cols = slice(P * (2 * j + c), P * (2 * j + c) + P)
+                    vcols = slice(P * c, P * c + P)
                     nc.tensor.matmul_mx(
                         out=pv_t[:, j, :],
-                        lhsT=codes[i][:, cols].bitcast(FP8X4),
-                        lhsT_scale=scales[i][:, cols],
-                        rhs=v_codes[:, g, cols].bitcast(FP8X4),
-                        rhs_scale=v_scales[:, g, cols],
+                        lhsT=codes[quad][:, cols].bitcast(FP8X4),
+                        lhsT_scale=scales[quad][:, cols],
+                        rhs=v_codes[:, g, vcols].bitcast(FP8X4),
+                        rhs_scale=v_scales[:, g, vcols],
                         start=(c == 0),
                         stop=(c == 1),
                     )
             pv[quad] = pv_t
 
-        def recip(quad):
+        def den_sum(quad):
             d_t = small.tile([P, 4], F32, tag="dsum")
             nc.vector.tensor_reduce(out=d_t[:], in_=den[quad][:], axis=AX.X, op=ALU.add)
+            dsum[quad] = d_t
+
+        def recip(quad):
             r_t = small.tile([P, 4], F32, tag="rden")
-            nc.vector.reciprocal(out=r_t[:], in_=d_t[:])
+            nc.vector.reciprocal(out=r_t[:], in_=dsum[quad][:])
             rden[quad] = r_t
 
         def p6(quad):
@@ -305,11 +315,12 @@ def tile_deepseekv4attention_kernel(tc, query, key, value, attention_mask, sinks
                 )
             nc.sync.dma_start(out=o_v[:, t, 4 * hq : 4 * hq + 4, :], in_=o_t[:])
 
-        nc.vector.tensor_copy(out=sink32[:], in_=sink_bf[:])
-        nc.vector.tensor_scalar(out=sinkc[:], in0=sink_bf[:], scalar1=RSCALE, scalar2=None, op0=ALU.mult)
-        prep_kt(0)
-        prep_qt(0)
-        prep_mask(0)
+        prep_kt_pe(0)
+        prep_kt_copy(0)
+        prep_qt_pe(0)
+        prep_qt_copy(0)
+        prep_mask_pe(0)
+        prep_mask_copy(0)
         prep_v(0)
 
         def quad_at(i, lag):
@@ -318,33 +329,48 @@ def tile_deepseekv4attention_kernel(tc, query, key, value, attention_mask, sinks
                 return last // 4
             return None
 
-        for i in range(-1, NU + 8):
-            q_mx = quad_at(i, 6)
-            q_out = quad_at(i, 7)
-            if 0 <= i - 2 < NU:
-                p3(i - 2)
+        mask_pe_at = {0: 1, 4: 2, 6: 3}
+        mask_copy_at = {1: 1, 5: 2, 7: 3}
+
+        for i in range(-1, NU + 11):
+            q_g = quad_at(i, 3)
+            q_z = quad_at(i, 8)
+            q_mx = quad_at(i, 9)
+            q_out = quad_at(i, 10)
+            if 0 <= i < NU:
+                stt(i)
+            if 0 <= i - 1 < NU:
+                tn(i - 1)
+                ex(i - 1)
             if i + 1 < NU:
                 qk(i + 1)
-            if 0 <= i - 3 < NU:
-                tr(i - 3)
-            if q_mx is not None:
-                recip(q_mx)
+            if 0 <= i - 2 < NU:
+                tr(i - 2)
             if 0 <= i < NU:
-                p1(i)
-            if 0 <= i - 1 < NU:
-                p2(i - 1)
-            if 0 <= i - 5 < NU:
-                p5(i - 5)
+                r1(i)
+                r0(i)
+            if q_z is not None:
+                den_sum(q_z)
+                quantise(q_z)
+                recip(q_z)
             if q_mx is not None:
                 mx(q_mx)
-            if 0 <= i - 4 < NU:
-                p4(i - 4)
+            if 0 <= i - 3 < NU:
+                p4(i - 3)
+            if q_g is not None:
+                regroup(q_g)
             if q_out is not None:
                 p6(q_out)
+            if (i + 6) % 8 == 0 and 0 < (i + 6) // 8 < NU // 8:
+                prep_qt_pe((i + 6) // 8)
             if (i + 5) % 8 == 0 and 0 < (i + 5) // 8 < NU // 8:
-                prep_qt((i + 5) // 8)
-            if i >= 0 and i % 4 == 0 and i // 4 + 1 < NT:
-                prep_mask(i // 4 + 1)
-            if i == 41:
-                prep_kt(1)
+                prep_qt_copy((i + 5) // 8)
+            if i in mask_pe_at:
+                prep_mask_pe(mask_pe_at[i])
+            if i in mask_copy_at:
+                prep_mask_copy(mask_copy_at[i])
+            if i == 46:
+                prep_kt_pe(1)
                 prep_v(1)
+            if i == 47:
+                prep_kt_copy(1)

@@ -21,6 +21,7 @@ HALF = S // 2
 NT = S // P
 NU = H * NT
 NQ = NU // 4
+NG = NQ - 2
 PAD = 8
 SCALE = 1.0 / (D ** 0.5)
 RSCALE = D ** 0.5
@@ -35,6 +36,7 @@ def tile_deepseekv4attention_kernel(tc, query, key, value, attention_mask, sinks
         e_pool = ctx.enter_context(tc.tile_pool(name="ep", bufs=3))
         pl_pool = ctx.enter_context(tc.tile_pool(name="plp", bufs=3))
         et_pool = ctx.enter_context(tc.tile_pool(name="etp", bufs=1))
+        etd_pool = ctx.enter_context(tc.tile_pool(name="etdp", bufs=2))
         c_pool = ctx.enter_context(tc.tile_pool(name="cp", bufs=2))
         small = ctx.enter_context(tc.tile_pool(name="small", bufs=4))
         o_pool = ctx.enter_context(tc.tile_pool(name="op", bufs=3))
@@ -69,9 +71,9 @@ def tile_deepseekv4attention_kernel(tc, query, key, value, attention_mask, sinks
 
         nc.scalar.dma_start(out=sink_bf[:], in_=sinks.partition_broadcast(P))
         nc.sync.dma_start(out=k_raw[:, 0], in_=k_v[:, 0])
-        for h in range(4):
-            nc.sync.dma_start(out=q_raw[:, h], in_=q_v[:, h])
+        nc.sync.dma_start(out=q_raw[:, 0:4, 0:2, :], in_=q_v[:, 0:4, 0:2, :])
         nc.sync.dma_start(out=mask_sb[:, 0:2, :], in_=m_v[:, 0:2, :])
+        nc.sync.dma_start(out=q_raw[:, 0:4, 2:NT, :], in_=q_v[:, 0:4, 2:NT, :])
         nc.sync.dma_start(out=v_raw[:, 0], in_=v_v[:, 0])
         nc.sync.dma_start(out=mask_sb[:, 2:4, :], in_=m_v[:, 2:4, :])
         nc.sync.dma_start(out=mask_sb[:, 4:8, :], in_=m_v[:, 4:8, :])
@@ -84,8 +86,11 @@ def tile_deepseekv4attention_kernel(tc, query, key, value, attention_mask, sinks
 
         x_ps = {}
 
-        def prep_kt_pe(g):
-            kt_ps = ps_x.tile([P, NT, P], BF16, tag="x")
+        def prep_kt_pe(g, first=False):
+            if first:
+                kt_ps = ps_t.tile([P, NT, P], BF16, tag="tr")
+            else:
+                kt_ps = ps_x.tile([P, NT, P], BF16, tag="x")
             for a in range(NT):
                 nc.tensor.transpose(out=kt_ps[:, a, :], in_=k_raw[:, g, a, :], identity=ident[:])
             x_ps["k%d" % g] = kt_ps
@@ -119,9 +124,12 @@ def tile_deepseekv4attention_kernel(tc, query, key, value, attention_mask, sinks
 
         qt_sb = {}
 
-        def prep_qt_pe(b):
+        def prep_qt_pe(b, first=False):
             hq, tp = divmod(b, 4)
-            q_ps = ps_x.tile([P, 8, P], BF16, tag="x")
+            if first:
+                q_ps = ps_t.tile([P, 8, P], BF16, tag="tr")
+            else:
+                q_ps = ps_x.tile([P, 8, P], BF16, tag="x")
             for t2 in range(2):
                 for j in range(4):
                     nc.tensor.transpose(
@@ -131,9 +139,12 @@ def tile_deepseekv4attention_kernel(tc, query, key, value, attention_mask, sinks
                     )
             x_ps["q%d" % b] = q_ps
 
-        def prep_qt_copy(b):
+        def prep_qt_copy(b, first=False):
             qt = qt_pool.tile([P, 8, P], BF16, tag="qtsb")
-            nc.scalar.copy(out=qt[:], in_=x_ps["q%d" % b][:])
+            if first:
+                nc.vector.tensor_copy(out=qt[:], in_=x_ps["q%d" % b][:])
+            else:
+                nc.scalar.copy(out=qt[:], in_=x_ps["q%d" % b][:])
             qt_sb[b] = qt
 
         sc_a = {}
@@ -249,6 +260,16 @@ def tile_deepseekv4attention_kernel(tc, query, key, value, attention_mask, sinks
 
         def p4(i):
             j = i % 4
+            if i // 4 >= NG:
+                if j == 0:
+                    etd_t = etd_pool.tile([P, 8, P, 4], BF16, tag="etd", align_bytes=64)
+                    et_sb[i // 4] = etd_t
+                src = tr_ps[i][:].rearrange("p (c t) q -> p c q t", t=4)
+                if j % 2 == 0:
+                    nc.scalar.copy(out=et_sb[i // 4][:, 2 * j : 2 * j + 2], in_=src)
+                else:
+                    nc.vector.tensor_copy(out=et_sb[i // 4][:, 2 * j : 2 * j + 2], in_=src)
+                return
             if j == 0:
                 pl_t = pl_pool.tile([P, 4, S], BF16, tag="plain")
                 plain[i // 4] = pl_t
@@ -277,10 +298,26 @@ def tile_deepseekv4attention_kernel(tc, query, key, value, attention_mask, sinks
             codes[quad] = c_t
             scales[quad] = sc_b
 
-        def mx(quad):
-            pv_t = ps_x.tile([P, 4, D], F32, tag="x")
+        def quantise_part(quad, j0, j1):
+            if j0 == 0:
+                c_t = c_pool.tile([P, 8 * P], U32, tag="codes", align_bytes=64)
+                sc_b = c_pool.tile([P, 8 * P], U8, tag="scales", align_bytes=64)
+                codes[quad] = c_t
+                scales[quad] = sc_b
+            cols = slice(2 * P * j0, 2 * P * j1)
+            nc.vector.quantize_mx(
+                out=codes[quad][:, cols].bitcast(FP8X4),
+                scales=scales[quad][:, cols],
+                in_=et_sb[quad][:, 2 * j0 : 2 * j1].rearrange("p c q t -> p (c q t)"),
+            )
+
+        def mx(quad, j0=0, j1=4):
+            if j0 == 0:
+                pv_t = ps_x.tile([P, 4, D], F32, tag="x")
+                pv[quad] = pv_t
+            pv_t = pv[quad]
             hq = where(4 * quad)[0]
-            for j in range(4):
+            for j in range(j0, j1):
                 g = (4 * hq + j) // (H // HKV)
                 for c in range(2):
                     cols = slice(P * (2 * j + c), P * (2 * j + c) + P)
@@ -294,7 +331,6 @@ def tile_deepseekv4attention_kernel(tc, query, key, value, attention_mask, sinks
                         start=(c == 0),
                         stop=(c == 1),
                     )
-            pv[quad] = pv_t
 
         def den_sum(quad):
             d_t = small.tile([P, 4], F32, tag="dsum")
@@ -306,39 +342,45 @@ def tile_deepseekv4attention_kernel(tc, query, key, value, attention_mask, sinks
             nc.vector.reciprocal(out=r_t[:], in_=dsum[quad][:])
             rden[quad] = r_t
 
-        def p6(quad):
-            hq, t, j0 = where(4 * quad)
-            o_t = o_pool.tile([P, 4, D], F32, tag="o")
-            for j in range(4):
+        o_sb = {}
+
+        def p6(quad, j0=0, j1=4):
+            hq, t, jz = where(4 * quad)
+            if j0 == 0:
+                o_t = o_pool.tile([P, 4, D], F32, tag="o")
+                o_sb[quad] = o_t
+            o_t = o_sb[quad]
+            for j in range(j0, j1):
                 nc.scalar.activation(
                     out=o_t[:, j, :], in_=pv[quad][:, j, :], func=ACT.Copy, scale=rden[quad][:, j : j + 1]
                 )
-            nc.sync.dma_start(out=o_v[:, t, 4 * hq : 4 * hq + 4, :], in_=o_t[:])
+            nc.sync.dma_start(out=o_v[:, t, 4 * hq + j0 : 4 * hq + j1, :], in_=o_t[:, j0:j1, :])
 
-        prep_kt_pe(0)
-        prep_kt_copy(0)
-        prep_qt_pe(0)
-        prep_qt_copy(0)
+        prep_kt_pe(0, first=True)
+        prep_qt_pe(0, first=True)
         prep_mask_pe(0)
+        prep_kt_copy(0)
+        prep_qt_copy(0, first=True)
         prep_mask_copy(0)
-        prep_v(0)
 
         def quad_at(i, lag):
             last = i - lag
-            if 0 <= last < NU and last % 4 == 3:
+            if 0 <= last < 4 * NG and last % 4 == 3:
                 return last // 4
             return None
 
-        mask_pe_at = {0: 1, 4: 2, 6: 3}
-        mask_copy_at = {1: 1, 5: 2, 7: 3}
+        mask_pe_at = {3: 1, 5: 2, 7: 3}
+        mask_copy_at = {4: 1, 6: 2, 8: 3}
 
-        for i in range(-1, NU + 11):
+        for i in range(-1, NU + 3):
             q_g = quad_at(i, 3)
-            q_z = quad_at(i, 8)
-            q_mx = quad_at(i, 9)
-            q_out = quad_at(i, 10)
+            q_z = quad_at(i, 7)
+            q_mx = quad_at(i, 8)
+            q_out = quad_at(i, 9)
             if 0 <= i < NU:
                 stt(i)
+            if i == NU:
+                quantise_part(NG, 0, 2)
             if 0 <= i - 1 < NU:
                 tn(i - 1)
                 ex(i - 1)
@@ -349,28 +391,49 @@ def tile_deepseekv4attention_kernel(tc, query, key, value, attention_mask, sinks
             if 0 <= i < NU:
                 r1(i)
                 r0(i)
+            if i == 3:
+                prep_v(0)
+            if i == 46:
+                prep_v(1)
             if q_z is not None:
                 den_sum(q_z)
                 quantise(q_z)
                 recip(q_z)
-            if q_mx is not None:
-                mx(q_mx)
-            if 0 <= i - 3 < NU:
-                p4(i - 3)
-            if q_g is not None:
-                regroup(q_g)
             if q_out is not None:
                 p6(q_out)
+            if q_mx is not None:
+                mx(q_mx)
+            if i == NU:
+                den_sum(NG)
+                quantise_part(NG, 2, 4)
+                recip(NG)
+            if i == NU + 1:
+                mx(NG)
+            if 0 <= i - 3 < NU:
+                p4(i - 3)
+            if i == NU + 1:
+                den_sum(NG + 1)
+                quantise_part(NG + 1, 0, 2)
+                recip(NG + 1)
+                p6(NG)
+            if i == NU + 2:
+                quantise_part(NG + 1, 2, 3)
+                mx(NG + 1, 0, 3)
+                p6(NG + 1, 0, 3)
+                quantise_part(NG + 1, 3, 4)
+                mx(NG + 1, 3, 4)
+                p6(NG + 1, 3, 4)
+            if q_g is not None:
+                regroup(q_g)
+            if (i + 7) % 8 == 0 and 0 < (i + 7) // 8 < NU // 8:
+                prep_qt_pe((i + 7) // 8)
             if (i + 6) % 8 == 0 and 0 < (i + 6) // 8 < NU // 8:
-                prep_qt_pe((i + 6) // 8)
-            if (i + 5) % 8 == 0 and 0 < (i + 5) // 8 < NU // 8:
-                prep_qt_copy((i + 5) // 8)
+                prep_qt_copy((i + 6) // 8)
             if i in mask_pe_at:
                 prep_mask_pe(mask_pe_at[i])
             if i in mask_copy_at:
                 prep_mask_copy(mask_copy_at[i])
-            if i == 46:
+            if i == 45:
                 prep_kt_pe(1)
-                prep_v(1)
-            if i == 47:
+            if i == 46:
                 prep_kt_copy(1)

@@ -21,7 +21,7 @@ HALF = S // 2
 NT = S // P
 NU = H * NT
 NQ = NU // 4
-NG = NQ - 2
+NG = NQ - 1
 PAD = 8
 SCALE = 1.0 / (D ** 0.5)
 RSCALE = D ** 0.5
@@ -34,9 +34,7 @@ def tile_deepseekv4attention_kernel(tc, query, key, value, attention_mask, sinks
         const = ctx.enter_context(tc.tile_pool(name="const", bufs=1))
         qt_pool = ctx.enter_context(tc.tile_pool(name="qtp", bufs=3))
         e_pool = ctx.enter_context(tc.tile_pool(name="ep", bufs=3))
-        pl_pool = ctx.enter_context(tc.tile_pool(name="plp", bufs=3))
-        et_pool = ctx.enter_context(tc.tile_pool(name="etp", bufs=1))
-        etd_pool = ctx.enter_context(tc.tile_pool(name="etdp", bufs=2))
+        et_pool = ctx.enter_context(tc.tile_pool(name="etp", bufs=3))
         c_pool = ctx.enter_context(tc.tile_pool(name="cp", bufs=2))
         small = ctx.enter_context(tc.tile_pool(name="small", bufs=4))
         o_pool = ctx.enter_context(tc.tile_pool(name="op", bufs=3))
@@ -49,14 +47,14 @@ def tile_deepseekv4attention_kernel(tc, query, key, value, attention_mask, sinks
         q_v = query[0].rearrange("h (p t) d -> p h t d", t=NT)
         m_v = attention_mask[0, 0].rearrange("(p t) k -> p t k", t=NT)
         k_v = key[0].rearrange("g (a p) d -> p g a d", p=P)
-        v_v = value[0].rearrange("g (a p) d -> p g a d", p=P)
+        v_v = value[0].rearrange("g (a p e) d -> p g a e d", p=P, e=2)
         o_v = out[0].rearrange("(p t) h d -> p t h d", t=NT)
 
         q_raw = const.tile([P, H, NT, D], BF16)
         mask_sb = const.tile([P, NT, S], BF16)
         mask_t = const.tile([P, NT, 4, P], F32)
         k_raw = const.tile([P, HKV, NT, D], BF16)
-        v_raw = const.tile([P, HKV, NT, D], BF16)
+        v_raw = const.tile([P, HKV, 4, 2, D], BF16)
         sink_bf = const.tile([P, H], BF16)
         kt_sb = const.tile([P, HKV, S], BF16)
         v_codes = const.tile([P, HKV, 2 * D], U32, align_bytes=64)
@@ -115,7 +113,7 @@ def tile_deepseekv4attention_kernel(tc, query, key, value, attention_mask, sinks
             )
 
         def prep_v(g):
-            nc.vector.tensor_copy(out=v_grouped[:], in_=v_raw[:, g].rearrange("p (c t) d -> p c d t", t=4))
+            nc.vector.tensor_copy(out=v_grouped[:], in_=v_raw[:, g].rearrange("p (c u) e d -> p c d (u e)", u=2))
             nc.vector.quantize_mx(
                 out=v_codes[:, g, :].bitcast(FP8X4),
                 scales=v_scales[:, g, :],
@@ -251,41 +249,24 @@ def tile_deepseekv4attention_kernel(tc, query, key, value, attention_mask, sinks
             e_sb[i] = e_t
 
         def tr(i):
-            tr_t = ps_t.tile([P, 8, P], BF16, tag="tr")
-            for a in range(8):
-                nc.tensor.transpose(
-                    out=tr_t[:, a, :], in_=e_sb[i][:, PAD + P * a : PAD + P * a + P], identity=ident[:]
-                )
+            tr_t = ps_t.tile([P, 4, P], F32, tag="tr")
+            words = e_sb[i][:, PAD : PAD + S].bitcast(F32)
+            for a in range(4):
+                nc.tensor.transpose(out=tr_t[:, a, :], in_=words[:, P * a : P * a + P], identity=ident32[:])
             tr_ps[i] = tr_t
 
         def p4(i):
             j = i % 4
-            if i // 4 >= NG:
-                if j == 0:
-                    etd_t = etd_pool.tile([P, 8, P, 4], BF16, tag="etd", align_bytes=64)
-                    et_sb[i // 4] = etd_t
-                src = tr_ps[i][:].rearrange("p (c t) q -> p c q t", t=4)
-                if j % 2 == 0:
-                    nc.scalar.copy(out=et_sb[i // 4][:, 2 * j : 2 * j + 2], in_=src)
-                else:
-                    nc.vector.tensor_copy(out=et_sb[i // 4][:, 2 * j : 2 * j + 2], in_=src)
-                return
             if j == 0:
-                pl_t = pl_pool.tile([P, 4, S], BF16, tag="plain")
-                plain[i // 4] = pl_t
-            nc.scalar.copy(out=plain[i // 4][:, j, :], in_=tr_ps[i][:].rearrange("p a q -> p (a q)"))
-
-        def regroup(quad):
-            et_t = et_pool.tile([P, 8, P, 4], BF16, tag="et", align_bytes=64)
-            nc.gpsimd.tensor_scalar(
-                out=et_t[:],
-                in0=plain[quad][:].rearrange("p j (c t q) -> p (j c) q t", c=2, t=4),
-                scalar1=1.0,
-                scalar2=0.0,
-                op0=ALU.mult,
-                op1=ALU.add,
-            )
-            et_sb[quad] = et_t
+                et_t = et_pool.tile([P, 8, P, 4], BF16, tag="et", align_bytes=64)
+                et_sb[i // 4] = et_t
+            et32 = et_sb[i // 4][:].rearrange("p c q t -> p (c q t)").bitcast(F32)
+            dst = et32[:, 2 * P * 2 * j : 2 * P * 2 * (j + 1)].rearrange("p (c q u) -> p c q u", c=2, u=2)
+            src = tr_ps[i][:].rearrange("p (c u) q -> p c q u", u=2)
+            if i // 4 == NG and j % 2 == 1:
+                nc.vector.tensor_copy(out=dst, in_=src)
+            else:
+                nc.scalar.copy(out=dst, in_=src)
 
         def quantise(quad):
             c_t = c_pool.tile([P, 8 * P], U32, tag="codes", align_bytes=64)
@@ -369,18 +350,15 @@ def tile_deepseekv4attention_kernel(tc, query, key, value, attention_mask, sinks
                 return last // 4
             return None
 
-        mask_pe_at = {3: 1, 5: 2, 7: 3}
-        mask_copy_at = {4: 1, 6: 2, 8: 3}
+        mask_pe_at = {2: 1, 4: 2, 6: 3}
+        mask_copy_at = {3: 1, 5: 2, 7: 3}
 
         for i in range(-1, NU + 3):
-            q_g = quad_at(i, 3)
-            q_z = quad_at(i, 7)
-            q_mx = quad_at(i, 8)
-            q_out = quad_at(i, 9)
+            q_z = quad_at(i, 4)
+            q_mx = quad_at(i, 5)
+            q_out = quad_at(i, 6)
             if 0 <= i < NU:
                 stt(i)
-            if i == NU:
-                quantise_part(NG, 0, 2)
             if 0 <= i - 1 < NU:
                 tn(i - 1)
                 ex(i - 1)
@@ -403,28 +381,19 @@ def tile_deepseekv4attention_kernel(tc, query, key, value, attention_mask, sinks
                 p6(q_out)
             if q_mx is not None:
                 mx(q_mx)
-            if i == NU:
-                den_sum(NG)
-                quantise_part(NG, 2, 4)
-                recip(NG)
-            if i == NU + 1:
-                mx(NG)
             if 0 <= i - 3 < NU:
                 p4(i - 3)
             if i == NU + 1:
-                den_sum(NG + 1)
-                quantise_part(NG + 1, 0, 2)
-                recip(NG + 1)
-                p6(NG)
+                quantise_part(NG, 0, 2)
             if i == NU + 2:
-                quantise_part(NG + 1, 2, 3)
-                mx(NG + 1, 0, 3)
-                p6(NG + 1, 0, 3)
-                quantise_part(NG + 1, 3, 4)
-                mx(NG + 1, 3, 4)
-                p6(NG + 1, 3, 4)
-            if q_g is not None:
-                regroup(q_g)
+                den_sum(NG)
+                quantise_part(NG, 2, 3)
+                recip(NG)
+                mx(NG, 0, 3)
+                p6(NG, 0, 3)
+                quantise_part(NG, 3, 4)
+                mx(NG, 3, 4)
+                p6(NG, 3, 4)
             if (i + 7) % 8 == 0 and 0 < (i + 7) // 8 < NU // 8:
                 prep_qt_pe((i + 7) // 8)
             if (i + 6) % 8 == 0 and 0 < (i + 6) // 8 < NU // 8:

@@ -21,26 +21,24 @@ HALF = S // 2
 NT = S // P
 NU = H * NT
 NQ = NU // 4
-NG = NQ - 1
-PAD = 8
 SCALE = 1.0 / (D ** 0.5)
 RSCALE = D ** 0.5
 FLOPS = 2 * 2 * H * S * S * D
+V_COPIES = (1, 3)
 
 
 def tile_deepseekv4attention_kernel(tc, query, key, value, attention_mask, sinks, out):
     nc = tc.nc
     with ExitStack() as ctx:
         const = ctx.enter_context(tc.tile_pool(name="const", bufs=1))
-        qt_pool = ctx.enter_context(tc.tile_pool(name="qtp", bufs=3))
-        e_pool = ctx.enter_context(tc.tile_pool(name="ep", bufs=3))
+        qt_pool = ctx.enter_context(tc.tile_pool(name="qtp", bufs=4))
+        e_pool = ctx.enter_context(tc.tile_pool(name="ep", bufs=4))
         et_pool = ctx.enter_context(tc.tile_pool(name="etp", bufs=3))
         c_pool = ctx.enter_context(tc.tile_pool(name="cp", bufs=2))
         small = ctx.enter_context(tc.tile_pool(name="small", bufs=4))
         o_pool = ctx.enter_context(tc.tile_pool(name="op", bufs=3))
-        ps_a = ctx.enter_context(tc.psum_pool(name="ps_a", bufs=2))
-        ps_c = ctx.enter_context(tc.psum_pool(name="ps_c", bufs=3))
-        ps_t = ctx.enter_context(tc.psum_pool(name="ps_t", bufs=2))
+        ps_s = ctx.enter_context(tc.psum_pool(name="ps_s", bufs=6))
+        ps_t = ctx.enter_context(tc.psum_pool(name="ps_t", bufs=1))
         ps_x = ctx.enter_context(tc.psum_pool(name="ps_x", bufs=1))
         ctx.enter_context(tc.manual_schedule())
 
@@ -52,17 +50,18 @@ def tile_deepseekv4attention_kernel(tc, query, key, value, attention_mask, sinks
 
         q_raw = const.tile([P, H, NT, D], BF16)
         mask_sb = const.tile([P, NT, S], BF16)
-        mask_t = const.tile([P, NT, 4, P], F32)
+        mask_t = const.tile([P, NT, 8, P], F32)
         k_raw = const.tile([P, HKV, NT, D], BF16)
         v_raw = const.tile([P, HKV, 4, 2, D], BF16)
         sink_bf = const.tile([P, H], BF16)
+        sink_f = const.tile([P, H], F32)
+        nsink = const.tile([P, H], F32)
         kt_sb = const.tile([P, HKV, S], BF16)
         v_codes = const.tile([P, HKV, 2 * D], U32, align_bytes=64)
         v_scales = const.tile([P, HKV, 2 * D], U8, align_bytes=64)
         v_grouped = const.tile([P, 2, D, 4], BF16, align_bytes=64)
         ident = const.tile([P, P], BF16)
         ident32 = const.tile([P, P], F32)
-        s_bufs = [const.tile([P, PAD + HALF], F32, name="s_buf%d" % j) for j in range(4)]
 
         make_identity(nc, ident[:])
         make_identity(nc, ident32[:])
@@ -72,8 +71,8 @@ def tile_deepseekv4attention_kernel(tc, query, key, value, attention_mask, sinks
         nc.sync.dma_start(out=q_raw[:, 0:4, 0:2, :], in_=q_v[:, 0:4, 0:2, :])
         nc.sync.dma_start(out=mask_sb[:, 0:2, :], in_=m_v[:, 0:2, :])
         nc.sync.dma_start(out=q_raw[:, 0:4, 2:NT, :], in_=q_v[:, 0:4, 2:NT, :])
-        nc.sync.dma_start(out=v_raw[:, 0], in_=v_v[:, 0])
         nc.sync.dma_start(out=mask_sb[:, 2:4, :], in_=m_v[:, 2:4, :])
+        nc.sync.dma_start(out=v_raw[:, 0], in_=v_v[:, 0])
         nc.sync.dma_start(out=mask_sb[:, 4:8, :], in_=m_v[:, 4:8, :])
         for h in range(4, 8):
             nc.sync.dma_start(out=q_raw[:, h], in_=q_v[:, h])
@@ -82,13 +81,16 @@ def tile_deepseekv4attention_kernel(tc, query, key, value, attention_mask, sinks
         for h in range(8, H):
             nc.sync.dma_start(out=q_raw[:, h], in_=q_v[:, h])
 
-        x_ps = {}
+        nc.gpsimd.tensor_copy(out=sink_f[:], in_=sink_bf[:])
+        nc.gpsimd.tensor_scalar(
+            out=nsink[:], in0=sink_bf[:], scalar1=-1.0, scalar2=0.0, op0=ALU.mult, op1=ALU.add
+        )
 
-        def prep_kt_pe(g, first=False):
-            if first:
-                kt_ps = ps_t.tile([P, NT, P], BF16, tag="tr")
-            else:
-                kt_ps = ps_x.tile([P, NT, P], BF16, tag="x")
+        x_ps = {}
+        qt_sb = {}
+
+        def prep_kt_pe(g, pool, tag):
+            kt_ps = pool.tile([P, NT, P], BF16, tag=tag, name="kt_ps")
             for a in range(NT):
                 nc.tensor.transpose(out=kt_ps[:, a, :], in_=k_raw[:, g, a, :], identity=ident[:])
             x_ps["k%d" % g] = kt_ps
@@ -96,21 +98,19 @@ def tile_deepseekv4attention_kernel(tc, query, key, value, attention_mask, sinks
         def prep_kt_copy(g):
             nc.scalar.copy(out=kt_sb[:, g, :], in_=x_ps["k%d" % g][:].rearrange("p a k -> p (a k)"))
 
-        def prep_mask_pe(tp):
-            mp = ps_x.tile([P, 2, 4, P], BF16, tag="x")
-            for t2 in range(2):
-                for a in range(4):
-                    nc.tensor.transpose(
-                        out=mp[:, t2, a, :],
-                        in_=mask_sb[:, 2 * tp + t2, HALF + P * a : HALF + P * a + P],
-                        identity=ident[:],
-                    )
-            x_ps["m%d" % tp] = mp
+        def prep_mask_pe(t, pool, tag, a0=0, a1=8):
+            mp = pool.tile([P, a1 - a0, P], BF16, tag=tag, name="mp_ps")
+            for a in range(a0, a1):
+                nc.tensor.transpose(out=mp[:, a - a0, :], in_=mask_sb[:, t, P * a : P * a + P], identity=ident[:])
+            x_ps["m%d_%d" % (t, a0)] = mp
 
-        def prep_mask_copy(tp):
-            nc.scalar.activation(
-                out=mask_t[:, 2 * tp : 2 * tp + 2], in_=x_ps["m%d" % tp][:], func=ACT.Copy, scale=RSCALE
-            )
+        def prep_mask_copy(t, a0=0, a1=8, on_vector=False):
+            src = x_ps["m%d_%d" % (t, a0)][:]
+            dst = mask_t[:, t, a0:a1, :]
+            if on_vector:
+                nc.vector.tensor_scalar(out=dst, in0=src, scalar1=RSCALE, scalar2=None, op0=ALU.mult)
+            else:
+                nc.scalar.activation(out=dst, in_=src, func=ACT.Copy, scale=RSCALE)
 
         def prep_v(g):
             nc.vector.tensor_copy(out=v_grouped[:], in_=v_raw[:, g].rearrange("p (c u) e d -> p c d (u e)", u=2))
@@ -120,14 +120,9 @@ def tile_deepseekv4attention_kernel(tc, query, key, value, attention_mask, sinks
                 in_=v_grouped[:].rearrange("p c d t -> p (c d t)"),
             )
 
-        qt_sb = {}
-
-        def prep_qt_pe(b, first=False):
+        def prep_qt_pe(b, pool, tag):
             hq, tp = divmod(b, 4)
-            if first:
-                q_ps = ps_t.tile([P, 8, P], BF16, tag="tr")
-            else:
-                q_ps = ps_x.tile([P, 8, P], BF16, tag="x")
+            q_ps = pool.tile([P, 8, P], BF16, tag=tag, name="q_ps")
             for t2 in range(2):
                 for j in range(4):
                     nc.tensor.transpose(
@@ -137,29 +132,26 @@ def tile_deepseekv4attention_kernel(tc, query, key, value, attention_mask, sinks
                     )
             x_ps["q%d" % b] = q_ps
 
-        def prep_qt_copy(b, first=False):
+        def prep_qt_copy(b, on_vector=False):
             qt = qt_pool.tile([P, 8, P], BF16, tag="qtsb")
-            if first:
+            if on_vector:
                 nc.vector.tensor_copy(out=qt[:], in_=x_ps["q%d" % b][:])
             else:
                 nc.scalar.copy(out=qt[:], in_=x_ps["q%d" % b][:])
             qt_sb[b] = qt
 
-        sc_a = {}
-        sc_c = {}
-        nm0 = {}
-        nm1 = {}
+        sc = {}
+        nmax = {}
         negm = {}
         den = {}
-        dsum = {}
         rden = {}
         e_sb = {}
         tr_ps = {}
-        plain = {}
         et_sb = {}
         codes = {}
         scales = {}
         pv = {}
+        o_sb = {}
 
         def where(i):
             hq, r = divmod(i, 4 * NT)
@@ -169,88 +161,76 @@ def tile_deepseekv4attention_kernel(tc, query, key, value, attention_mask, sinks
         def qk(i):
             hq, t, j = where(i)
             g = (4 * hq + j) // (H // HKV)
-            c_t = ps_c.tile([P, HALF], F32, tag="scc")
-            nc.tensor.matmul(
-                out=c_t[:], lhsT=qt_sb[i // 8][:, i % 8, :], rhs=kt_sb[:, g, HALF:S], start=True, stop=False
-            )
-            for a in range(4):
+            for c in range(2):
+                s_t = ps_s.tile([P, HALF], F32, tag="sc")
                 nc.tensor.matmul(
-                    out=c_t[:, P * a : P * a + P],
-                    lhsT=mask_t[:, t, a, :],
-                    rhs=ident32[:],
-                    is_transpose=True,
-                    start=False,
-                    stop=(a == 3),
+                    out=s_t[:],
+                    lhsT=qt_sb[i // 8][:, i % 8, :],
+                    rhs=kt_sb[:, g, HALF * c : HALF * c + HALF],
+                    start=True,
+                    stop=False,
                 )
-            sc_c[i] = c_t
-            a_t = ps_a.tile([P, HALF], F32, tag="sca")
-            nc.tensor.matmul(
-                out=a_t[:], lhsT=qt_sb[i // 8][:, i % 8, :], rhs=kt_sb[:, g, 0:HALF], start=True, stop=True
-            )
-            sc_a[i] = a_t
+                for a in range(4):
+                    nc.tensor.matmul(
+                        out=s_t[:, P * a : P * a + P],
+                        lhsT=mask_t[:, t, 4 * c + a, :],
+                        rhs=ident32[:],
+                        is_transpose=True,
+                        start=False,
+                        stop=(a == 3),
+                    )
+                sc[i, c] = s_t
 
-        def stt(i):
-            hq, t, j = where(i)
-            h = 4 * hq + j
-            s_t = s_bufs[j]
-            if t == 0:
-                nc.vector.tensor_copy(out=s_t[:, PAD - 1 : PAD], in_=sink_bf[:, h : h + 1])
-            nc.vector.scalar_tensor_tensor(
-                out=s_t[:, PAD : PAD + HALF],
-                in0=sc_a[i][:],
-                scalar=SCALE,
-                in1=mask_sb[:, t, 0:HALF],
-                op0=ALU.mult,
-                op1=ALU.add,
-            )
-
-        def r1(i):
-            n_t = small.tile([P, 1], F32, tag="nm1")
-            nc.vector.tensor_reduce(out=n_t[:], in_=sc_c[i][:], axis=AX.X, op=ALU.max, negate=True)
-            nm1[i] = n_t
-
-        def r0(i):
-            n_t = small.tile([P, 1], F32, tag="nm0")
-            nc.vector.tensor_reduce(
-                out=n_t[:], in_=s_bufs[i % 4][:, PAD - 1 : PAD + HALF], axis=AX.X, op=ALU.max, negate=True
-            )
-            nm0[i] = n_t
+        def rmax(i, c):
+            n_t = small.tile([P, 1], F32, tag="nmax%d" % c, name="nm_t")
+            nc.vector.tensor_reduce(out=n_t[:], in_=sc[i, c][:], axis=AX.X, op=ALU.max, negate=True)
+            nmax[i, c] = n_t
 
         def tn(i):
-            n_t = small.tile([P, 1], F32, tag="negm")
-            nc.vector.tensor_scalar(
-                out=n_t[:], in0=nm1[i][:], scalar1=SCALE, scalar2=nm0[i][:], op0=ALU.mult, op1=ALU.min
+            hq, t, j = where(i)
+            h = 4 * hq + j
+            if j == 0:
+                n4_t = small.tile([P, 4], F32, tag="negm")
+                negm[i // 4] = n4_t
+            t_t = small.tile([P, 1], F32, tag="tmp")
+            nc.gpsimd.tensor_scalar(
+                out=t_t[:], in0=nmax[i, 0][:], scalar1=nmax[i, 1][:], scalar2=SCALE, op0=ALU.min, op1=ALU.mult
             )
-            negm[i] = n_t
+            nc.gpsimd.tensor_scalar(
+                out=negm[i // 4][:, j : j + 1],
+                in0=t_t[:],
+                scalar1=nsink[:, h : h + 1],
+                scalar2=0.0,
+                op0=ALU.min,
+                op1=ALU.add,
+            )
 
         def ex(i):
             j = i % 4
             if j == 0:
-                den_t = small.tile([P, 4, 2], F32, tag="den")
+                den_t = small.tile([P, 4, 3], F32, tag="den")
                 den[i // 4] = den_t
-            den_t = den[i // 4]
-            e_t = e_pool.tile([P, PAD + S], BF16, tag="e")
-            nc.scalar.activation(
-                out=e_t[:, PAD + HALF : PAD + S],
-                in_=sc_c[i][:],
-                func=ACT.Exp,
-                bias=negm[i][:],
-                scale=SCALE,
-                accum_out=den_t[:, j, 1:2],
-            )
-            nc.scalar.activation(
-                out=e_t[:, PAD - 1 : PAD + HALF],
-                in_=s_bufs[j][:, PAD - 1 : PAD + HALF],
-                func=ACT.Exp,
-                bias=negm[i][:],
-                scale=1.0,
-                accum_out=den_t[:, j, 0:1],
-            )
+            e_t = e_pool.tile([P, S], BF16, tag="e")
+            for c in range(2):
+                nc.scalar.activation(
+                    out=e_t[:, HALF * c : HALF * c + HALF],
+                    in_=sc[i, c][:],
+                    func=ACT.Exp,
+                    bias=negm[i // 4][:, j : j + 1],
+                    scale=SCALE,
+                    accum_out=den[i // 4][:, j, c : c + 1],
+                )
             e_sb[i] = e_t
+
+        def sink_term(quad):
+            hq, t, jz = where(4 * quad)
+            d_t = small.tile([P, 4], F32, tag="sdiff")
+            nc.gpsimd.tensor_tensor(out=d_t[:], in0=negm[quad][:], in1=sink_f[:, 4 * hq : 4 * hq + 4], op=ALU.add)
+            nc.scalar.activation(out=den[quad][:, :, 2], in_=d_t[:], func=ACT.Exp)
 
         def tr(i):
             tr_t = ps_t.tile([P, 4, P], F32, tag="tr")
-            words = e_sb[i][:, PAD : PAD + S].bitcast(F32)
+            words = e_sb[i][:].bitcast(F32)
             for a in range(4):
                 nc.tensor.transpose(out=tr_t[:, a, :], in_=words[:, P * a : P * a + P], identity=ident32[:])
             tr_ps[i] = tr_t
@@ -261,25 +241,14 @@ def tile_deepseekv4attention_kernel(tc, query, key, value, attention_mask, sinks
                 et_t = et_pool.tile([P, 8, P, 4], BF16, tag="et", align_bytes=64)
                 et_sb[i // 4] = et_t
             et32 = et_sb[i // 4][:].rearrange("p c q t -> p (c q t)").bitcast(F32)
-            dst = et32[:, 2 * P * 2 * j : 2 * P * 2 * (j + 1)].rearrange("p (c q u) -> p c q u", c=2, u=2)
+            dst = et32[:, 4 * P * j : 4 * P * (j + 1)].rearrange("p (c q u) -> p c q u", c=2, u=2)
             src = tr_ps[i][:].rearrange("p (c u) q -> p c q u", u=2)
-            if i // 4 == NG and j % 2 == 1:
+            if j in V_COPIES:
                 nc.vector.tensor_copy(out=dst, in_=src)
             else:
                 nc.scalar.copy(out=dst, in_=src)
 
-        def quantise(quad):
-            c_t = c_pool.tile([P, 8 * P], U32, tag="codes", align_bytes=64)
-            sc_b = c_pool.tile([P, 8 * P], U8, tag="scales", align_bytes=64)
-            nc.vector.quantize_mx(
-                out=c_t[:].bitcast(FP8X4),
-                scales=sc_b[:],
-                in_=et_sb[quad][:].rearrange("p c q t -> p (c q t)"),
-            )
-            codes[quad] = c_t
-            scales[quad] = sc_b
-
-        def quantise_part(quad, j0, j1):
+        def quantise(quad, j0=0, j1=4):
             if j0 == 0:
                 c_t = c_pool.tile([P, 8 * P], U32, tag="codes", align_bytes=64)
                 sc_b = c_pool.tile([P, 8 * P], U8, tag="scales", align_bytes=64)
@@ -313,17 +282,12 @@ def tile_deepseekv4attention_kernel(tc, query, key, value, attention_mask, sinks
                         stop=(c == 1),
                     )
 
-        def den_sum(quad):
+        def recip(quad):
             d_t = small.tile([P, 4], F32, tag="dsum")
             nc.vector.tensor_reduce(out=d_t[:], in_=den[quad][:], axis=AX.X, op=ALU.add)
-            dsum[quad] = d_t
-
-        def recip(quad):
             r_t = small.tile([P, 4], F32, tag="rden")
-            nc.vector.reciprocal(out=r_t[:], in_=dsum[quad][:])
+            nc.vector.reciprocal(out=r_t[:], in_=d_t[:])
             rden[quad] = r_t
-
-        o_sb = {}
 
         def p6(quad, j0=0, j1=4):
             hq, t, jz = where(4 * quad)
@@ -337,72 +301,76 @@ def tile_deepseekv4attention_kernel(tc, query, key, value, attention_mask, sinks
                 )
             nc.sync.dma_start(out=o_v[:, t, 4 * hq + j0 : 4 * hq + j1, :], in_=o_t[:, j0:j1, :])
 
-        prep_kt_pe(0, first=True)
-        prep_qt_pe(0, first=True)
-        prep_mask_pe(0)
+        prep_kt_pe(0, ps_s, "sc")
+        prep_qt_pe(0, ps_s, "sc")
+        prep_mask_pe(0, ps_s, "sc", 0, 4)
+        prep_mask_pe(0, ps_s, "sc", 4, 8)
         prep_kt_copy(0)
-        prep_qt_copy(0, first=True)
-        prep_mask_copy(0)
+        prep_qt_copy(0, on_vector=True)
+        prep_mask_copy(0, 0, 4)
+        prep_mask_copy(0, 4, 8, on_vector=True)
+
+        prep_at = {-1: ("m", 1), 1: ("q", 1), 3: ("m", 2), 5: ("m", 3), 6: ("q", 2)}
+        prep_at.update({9: ("m", 4), 13: ("q", 3), 17: ("m", 5), 21: ("m", 6), 25: ("m", 7), 33: ("k", 1)})
+        for b in range(4, NU // 8):
+            prep_at[8 * b - 3] = ("q", b)
 
         def quad_at(i, lag):
             last = i - lag
-            if 0 <= last < 4 * NG and last % 4 == 3:
+            if 0 <= last < NU - 4 and last % 4 == 3:
                 return last // 4
             return None
 
-        mask_pe_at = {2: 1, 4: 2, 6: 3}
-        mask_copy_at = {3: 1, 5: 2, 7: 3}
-
         for i in range(-1, NU + 3):
+            q_s = quad_at(i, 2)
             q_z = quad_at(i, 4)
             q_mx = quad_at(i, 5)
             q_out = quad_at(i, 6)
+            if 0 <= i - 3 < NU:
+                p4(i - 3)
             if 0 <= i < NU:
-                stt(i)
-            if 0 <= i - 1 < NU:
-                tn(i - 1)
-                ex(i - 1)
+                rmax(i, 0)
+            if q_z is not None:
+                recip(q_z)
+                quantise(q_z)
+            if 0 <= i < NU:
+                rmax(i, 1)
+                tn(i)
+            if i in (3, 46):
+                prep_v(0 if i == 3 else 1)
             if i + 1 < NU:
                 qk(i + 1)
             if 0 <= i - 2 < NU:
                 tr(i - 2)
-            if 0 <= i < NU:
-                r1(i)
-                r0(i)
-            if i == 3:
-                prep_v(0)
-            if i == 46:
-                prep_v(1)
-            if q_z is not None:
-                den_sum(q_z)
-                quantise(q_z)
-                recip(q_z)
+            if 0 <= i - 1 < NU:
+                ex(i - 1)
+            if q_s is not None:
+                sink_term(q_s)
             if q_out is not None:
                 p6(q_out)
             if q_mx is not None:
                 mx(q_mx)
-            if 0 <= i - 3 < NU:
-                p4(i - 3)
             if i == NU + 1:
-                quantise_part(NG, 0, 2)
+                sink_term(NQ - 1)
+                quantise(NQ - 1, 0, 2)
+                recip(NQ - 1)
             if i == NU + 2:
-                den_sum(NG)
-                quantise_part(NG, 2, 3)
-                recip(NG)
-                mx(NG, 0, 3)
-                p6(NG, 0, 3)
-                quantise_part(NG, 3, 4)
-                mx(NG, 3, 4)
-                p6(NG, 3, 4)
-            if (i + 7) % 8 == 0 and 0 < (i + 7) // 8 < NU // 8:
-                prep_qt_pe((i + 7) // 8)
-            if (i + 6) % 8 == 0 and 0 < (i + 6) // 8 < NU // 8:
-                prep_qt_copy((i + 6) // 8)
-            if i in mask_pe_at:
-                prep_mask_pe(mask_pe_at[i])
-            if i in mask_copy_at:
-                prep_mask_copy(mask_copy_at[i])
-            if i == 45:
-                prep_kt_pe(1)
-            if i == 46:
-                prep_kt_copy(1)
+                quantise(NQ - 1, 2, 4)
+                mx(NQ - 1)
+                p6(NQ - 1)
+            if i - 1 in prep_at:
+                kind, b = prep_at[i - 1]
+                if kind == "m":
+                    prep_mask_copy(b)
+                elif kind == "q":
+                    prep_qt_copy(b)
+                else:
+                    prep_kt_copy(b)
+            if i in prep_at:
+                kind, b = prep_at[i]
+                if kind == "m":
+                    prep_mask_pe(b, ps_x, "x")
+                elif kind == "q":
+                    prep_qt_pe(b, ps_x, "x")
+                else:
+                    prep_kt_pe(b, ps_x, "x")

@@ -24,7 +24,7 @@ NQ = NU // 4
 SCALE = 1.0 / (D ** 0.5)
 RSCALE = D ** 0.5
 FLOPS = 2 * 2 * H * S * S * D
-V_COPIES = (1, 3)
+V_COPIES = (3,)
 
 
 def tile_deepseekv4attention_kernel(tc, query, key, value, attention_mask, sinks, out):
@@ -89,23 +89,21 @@ def tile_deepseekv4attention_kernel(tc, query, key, value, attention_mask, sinks
         x_ps = {}
         qt_sb = {}
 
-        def prep_kt_pe(g, pool, tag):
-            kt_ps = pool.tile([P, NT, P], BF16, tag=tag, name="kt_ps")
+        def prep_kt_pe(g, kt_ps):
             for a in range(NT):
                 nc.tensor.transpose(out=kt_ps[:, a, :], in_=k_raw[:, g, a, :], identity=ident[:])
-            x_ps["k%d" % g] = kt_ps
+            x_ps["k%d" % g] = kt_ps[:]
 
         def prep_kt_copy(g):
-            nc.scalar.copy(out=kt_sb[:, g, :], in_=x_ps["k%d" % g][:].rearrange("p a k -> p (a k)"))
+            nc.scalar.copy(out=kt_sb[:, g, :], in_=x_ps["k%d" % g].rearrange("p a k -> p (a k)"))
 
-        def prep_mask_pe(t, pool, tag, a0=0, a1=8):
-            mp = pool.tile([P, a1 - a0, P], BF16, tag=tag, name="mp_ps")
+        def prep_mask_pe(t, mp, a0=0, a1=8):
             for a in range(a0, a1):
                 nc.tensor.transpose(out=mp[:, a - a0, :], in_=mask_sb[:, t, P * a : P * a + P], identity=ident[:])
-            x_ps["m%d_%d" % (t, a0)] = mp
+            x_ps["m%d_%d" % (t, a0)] = mp[:, 0 : a1 - a0, :]
 
         def prep_mask_copy(t, a0=0, a1=8, on_vector=False):
-            src = x_ps["m%d_%d" % (t, a0)][:]
+            src = x_ps["m%d_%d" % (t, a0)]
             dst = mask_t[:, t, a0:a1, :]
             if on_vector:
                 nc.vector.tensor_scalar(out=dst, in0=src, scalar1=RSCALE, scalar2=None, op0=ALU.mult)
@@ -120,9 +118,8 @@ def tile_deepseekv4attention_kernel(tc, query, key, value, attention_mask, sinks
                 in_=v_grouped[:].rearrange("p c d t -> p (c d t)"),
             )
 
-        def prep_qt_pe(b, pool, tag):
+        def prep_qt_pe(b, q_ps):
             hq, tp = divmod(b, 4)
-            q_ps = pool.tile([P, 8, P], BF16, tag=tag, name="q_ps")
             for t2 in range(2):
                 for j in range(4):
                     nc.tensor.transpose(
@@ -130,14 +127,14 @@ def tile_deepseekv4attention_kernel(tc, query, key, value, attention_mask, sinks
                         in_=q_raw[:, 4 * hq + j, 2 * tp + t2, :],
                         identity=ident[:],
                     )
-            x_ps["q%d" % b] = q_ps
+            x_ps["q%d" % b] = q_ps[:]
 
         def prep_qt_copy(b, on_vector=False):
             qt = qt_pool.tile([P, 8, P], BF16, tag="qtsb")
             if on_vector:
-                nc.vector.tensor_copy(out=qt[:], in_=x_ps["q%d" % b][:])
+                nc.vector.tensor_copy(out=qt[:], in_=x_ps["q%d" % b])
             else:
-                nc.scalar.copy(out=qt[:], in_=x_ps["q%d" % b][:])
+                nc.scalar.copy(out=qt[:], in_=x_ps["q%d" % b])
             qt_sb[b] = qt
 
         sc = {}
@@ -170,16 +167,17 @@ def tile_deepseekv4attention_kernel(tc, query, key, value, attention_mask, sinks
                     start=True,
                     stop=False,
                 )
-                for a in range(4):
-                    nc.tensor.matmul(
-                        out=s_t[:, P * a : P * a + P],
-                        lhsT=mask_t[:, t, 4 * c + a, :],
-                        rhs=ident32[:],
-                        is_transpose=True,
-                        start=False,
-                        stop=(a == 3),
-                    )
                 sc[i, c] = s_t
+            for a in range(8):
+                c, a4 = divmod(a, 4)
+                nc.tensor.matmul(
+                    out=sc[i, c][:, P * a4 : P * a4 + P],
+                    lhsT=mask_t[:, t, a, :],
+                    rhs=ident32[:],
+                    is_transpose=True,
+                    start=False,
+                    stop=(a4 == 3),
+                )
 
         def rmax(i, c):
             n_t = small.tile([P, 1], F32, tag="nmax%d" % c, name="nm_t")
@@ -295,16 +293,19 @@ def tile_deepseekv4attention_kernel(tc, query, key, value, attention_mask, sinks
                 o_t = o_pool.tile([P, 4, D], F32, tag="o")
                 o_sb[quad] = o_t
             o_t = o_sb[quad]
-            for j in range(j0, j1):
-                nc.scalar.activation(
-                    out=o_t[:, j, :], in_=pv[quad][:, j, :], func=ACT.Copy, scale=rden[quad][:, j : j + 1]
-                )
+            nc.vector.tensor_tensor(
+                out=o_t[:, j0:j1, :],
+                in0=pv[quad][:, j0:j1, :],
+                in1=rden[quad][:, j0:j1].unsqueeze(2).to_broadcast([P, j1 - j0, D]),
+                op=ALU.mult,
+            )
             nc.sync.dma_start(out=o_v[:, t, 4 * hq + j0 : 4 * hq + j1, :], in_=o_t[:, j0:j1, :])
 
-        prep_kt_pe(0, ps_s, "sc")
-        prep_qt_pe(0, ps_s, "sc")
-        prep_mask_pe(0, ps_s, "sc", 0, 4)
-        prep_mask_pe(0, ps_s, "sc", 4, 8)
+        head_ps = [ps_s.tile([P, 8, P], BF16, tag="sc", name="head_ps") for n in range(4)]
+        prep_kt_pe(0, head_ps[0])
+        prep_qt_pe(0, head_ps[1])
+        prep_mask_pe(0, head_ps[2], 0, 4)
+        prep_mask_pe(0, head_ps[3], 4, 8)
         prep_kt_copy(0)
         prep_qt_copy(0, on_vector=True)
         prep_mask_copy(0, 0, 4)
@@ -328,6 +329,8 @@ def tile_deepseekv4attention_kernel(tc, query, key, value, attention_mask, sinks
             q_out = quad_at(i, 6)
             if 0 <= i - 3 < NU:
                 p4(i - 3)
+            if q_out is not None:
+                p6(q_out)
             if 0 <= i < NU:
                 rmax(i, 0)
             if q_z is not None:
@@ -338,6 +341,8 @@ def tile_deepseekv4attention_kernel(tc, query, key, value, attention_mask, sinks
                 tn(i)
             if i in (3, 46):
                 prep_v(0 if i == 3 else 1)
+            if q_mx is not None:
+                mx(q_mx)
             if i + 1 < NU:
                 qk(i + 1)
             if 0 <= i - 2 < NU:
@@ -346,10 +351,6 @@ def tile_deepseekv4attention_kernel(tc, query, key, value, attention_mask, sinks
                 ex(i - 1)
             if q_s is not None:
                 sink_term(q_s)
-            if q_out is not None:
-                p6(q_out)
-            if q_mx is not None:
-                mx(q_mx)
             if i == NU + 1:
                 sink_term(NQ - 1)
                 quantise(NQ - 1, 0, 2)
@@ -368,9 +369,10 @@ def tile_deepseekv4attention_kernel(tc, query, key, value, attention_mask, sinks
                     prep_kt_copy(b)
             if i in prep_at:
                 kind, b = prep_at[i]
+                prep_ps = ps_x.tile([P, 8, P], BF16, tag="x")
                 if kind == "m":
-                    prep_mask_pe(b, ps_x, "x")
+                    prep_mask_pe(b, prep_ps)
                 elif kind == "q":
-                    prep_qt_pe(b, ps_x, "x")
+                    prep_qt_pe(b, prep_ps)
                 else:
-                    prep_kt_pe(b, ps_x, "x")
+                    prep_kt_pe(b, prep_ps)

@@ -34,7 +34,7 @@ def tile_deepseekv4attention_kernel(tc, query, key, value, attention_mask, sinks
         qt_pool = ctx.enter_context(tc.tile_pool(name="qtp", bufs=4))
         e_pool = ctx.enter_context(tc.tile_pool(name="ep", bufs=4))
         et_pool = ctx.enter_context(tc.tile_pool(name="etp", bufs=3))
-        c_pool = ctx.enter_context(tc.tile_pool(name="cp", bufs=2))
+        c_pool = ctx.enter_context(tc.tile_pool(name="cp", bufs=3))
         small = ctx.enter_context(tc.tile_pool(name="small", bufs=4))
         o_pool = ctx.enter_context(tc.tile_pool(name="op", bufs=3))
         ps_s = ctx.enter_context(tc.psum_pool(name="ps_s", bufs=6))
@@ -141,6 +141,7 @@ def tile_deepseekv4attention_kernel(tc, query, key, value, attention_mask, sinks
         nmax = {}
         negm = {}
         den = {}
+        dsum = {}
         rden = {}
         e_sb = {}
         tr_ps = {}
@@ -223,8 +224,13 @@ def tile_deepseekv4attention_kernel(tc, query, key, value, attention_mask, sinks
         def sink_term(quad):
             hq, t, jz = where(4 * quad)
             d_t = small.tile([P, 4], F32, tag="sdiff")
+            sum_t = small.tile([P, 4], F32, tag="esum")
+            dsum_t = small.tile([P, 4], F32, tag="dsum")
             nc.gpsimd.tensor_tensor(out=d_t[:], in0=negm[quad][:], in1=sink_f[:, 4 * hq : 4 * hq + 4], op=ALU.add)
+            nc.gpsimd.tensor_tensor(out=sum_t[:], in0=den[quad][:, :, 0], in1=den[quad][:, :, 1], op=ALU.add)
             nc.scalar.activation(out=den[quad][:, :, 2], in_=d_t[:], func=ACT.Exp)
+            nc.gpsimd.tensor_tensor(out=dsum_t[:], in0=sum_t[:], in1=den[quad][:, :, 2], op=ALU.add)
+            dsum[quad] = dsum_t
 
         def tr(i):
             tr_t = ps_t.tile([P, 4, P], F32, tag="tr")
@@ -246,17 +252,18 @@ def tile_deepseekv4attention_kernel(tc, query, key, value, attention_mask, sinks
             else:
                 nc.scalar.copy(out=dst, in_=src)
 
-        def quantise(quad, j0=0, j1=4):
-            if j0 == 0:
+        def quantise(i):
+            quad, j = divmod(i, 4)
+            if j == 0:
                 c_t = c_pool.tile([P, 8 * P], U32, tag="codes", align_bytes=64)
                 sc_b = c_pool.tile([P, 8 * P], U8, tag="scales", align_bytes=64)
                 codes[quad] = c_t
                 scales[quad] = sc_b
-            cols = slice(2 * P * j0, 2 * P * j1)
+            cols = slice(2 * P * j, 2 * P * (j + 1))
             nc.vector.quantize_mx(
                 out=codes[quad][:, cols].bitcast(FP8X4),
                 scales=scales[quad][:, cols],
-                in_=et_sb[quad][:, 2 * j0 : 2 * j1].rearrange("p c q t -> p (c q t)"),
+                in_=et_sb[quad][:, 2 * j : 2 * j + 2].rearrange("p c q t -> p (c q t)"),
             )
 
         def mx(quad, j0=0, j1=4):
@@ -281,10 +288,8 @@ def tile_deepseekv4attention_kernel(tc, query, key, value, attention_mask, sinks
                     )
 
         def recip(quad):
-            d_t = small.tile([P, 4], F32, tag="dsum")
-            nc.vector.tensor_reduce(out=d_t[:], in_=den[quad][:], axis=AX.X, op=ALU.add)
             r_t = small.tile([P, 4], F32, tag="rden")
-            nc.vector.reciprocal(out=r_t[:], in_=d_t[:])
+            nc.vector.reciprocal(out=r_t[:], in_=dsum[quad][:])
             rden[quad] = r_t
 
         def p6(quad, j0=0, j1=4):
@@ -311,7 +316,7 @@ def tile_deepseekv4attention_kernel(tc, query, key, value, attention_mask, sinks
         prep_mask_copy(0, 0, 4)
         prep_mask_copy(0, 4, 8, on_vector=True)
 
-        prep_at = {-1: ("m", 1), 1: ("q", 1), 3: ("m", 2), 5: ("m", 3), 6: ("q", 2)}
+        prep_at = {-1: ("m", 1), 1: ("q", 1), 2: ("m", 2), 4: ("m", 3), 5: ("q", 2)}
         prep_at.update({9: ("m", 4), 13: ("q", 3), 17: ("m", 5), 21: ("m", 6), 25: ("m", 7), 33: ("k", 1)})
         for b in range(4, NU // 8):
             prep_at[8 * b - 3] = ("q", b)
@@ -324,25 +329,27 @@ def tile_deepseekv4attention_kernel(tc, query, key, value, attention_mask, sinks
 
         for i in range(-1, NU + 3):
             q_s = quad_at(i, 2)
-            q_z = quad_at(i, 4)
-            q_mx = quad_at(i, 5)
+            q_r = quad_at(i, 4)
+            q_mx1 = quad_at(i, 5)
             q_out = quad_at(i, 6)
             if 0 <= i - 3 < NU:
                 p4(i - 3)
             if q_out is not None:
                 p6(q_out)
+            if 0 <= i - 4 < NU:
+                quantise(i - 4)
             if 0 <= i < NU:
                 rmax(i, 0)
-            if q_z is not None:
-                recip(q_z)
-                quantise(q_z)
-            if 0 <= i < NU:
                 rmax(i, 1)
                 tn(i)
+            if q_r is not None:
+                recip(q_r)
             if i in (3, 46):
                 prep_v(0 if i == 3 else 1)
-            if q_mx is not None:
-                mx(q_mx)
+            if q_r is not None:
+                mx(q_r, 0, 2)
+            if q_mx1 is not None:
+                mx(q_mx1, 2, 4)
             if i + 1 < NU:
                 qk(i + 1)
             if 0 <= i - 2 < NU:
@@ -353,11 +360,11 @@ def tile_deepseekv4attention_kernel(tc, query, key, value, attention_mask, sinks
                 sink_term(q_s)
             if i == NU + 1:
                 sink_term(NQ - 1)
-                quantise(NQ - 1, 0, 2)
-                recip(NQ - 1)
             if i == NU + 2:
-                quantise(NQ - 1, 2, 4)
-                mx(NQ - 1)
+                recip(NQ - 1)
+                mx(NQ - 1, 0, 3)
+                quantise(NU - 1)
+                mx(NQ - 1, 3, 4)
                 p6(NQ - 1)
             if i - 1 in prep_at:
                 kind, b = prep_at[i - 1]

@@ -24,7 +24,10 @@ NQ = NU // 4
 SCALE = 1.0 / (D ** 0.5)
 RSCALE = D ** 0.5
 FLOPS = 2 * 2 * H * S * S * D
-V_COPIES = (3,)
+
+
+def copy_on_vector(i):
+    return i % 4 == 3
 
 
 def tile_deepseekv4attention_kernel(tc, query, key, value, attention_mask, sinks, out):
@@ -68,18 +71,17 @@ def tile_deepseekv4attention_kernel(tc, query, key, value, attention_mask, sinks
 
         nc.scalar.dma_start(out=sink_bf[:], in_=sinks.partition_broadcast(P))
         nc.sync.dma_start(out=k_raw[:, 0], in_=k_v[:, 0])
-        nc.sync.dma_start(out=q_raw[:, 0:4, 0:2, :], in_=q_v[:, 0:4, 0:2, :])
-        nc.sync.dma_start(out=mask_sb[:, 0:2, :], in_=m_v[:, 0:2, :])
-        nc.sync.dma_start(out=q_raw[:, 0:4, 2:NT, :], in_=q_v[:, 0:4, 2:NT, :])
-        nc.sync.dma_start(out=mask_sb[:, 2:4, :], in_=m_v[:, 2:4, :])
-        nc.sync.dma_start(out=v_raw[:, 0], in_=v_v[:, 0])
-        nc.sync.dma_start(out=mask_sb[:, 4:8, :], in_=m_v[:, 4:8, :])
-        for h in range(4, 8):
-            nc.sync.dma_start(out=q_raw[:, h], in_=q_v[:, h])
+        nc.sync.dma_start(out=q_raw[:, 0:8, 0, :], in_=q_v[:, 0:8, 0, :])
+        nc.sync.dma_start(out=mask_sb[:, 0, :], in_=m_v[:, 0, :])
+        nc.sync.dma_start(out=q_raw[:, 8:16, 0, :], in_=q_v[:, 8:16, 0, :])
         nc.sync.dma_start(out=k_raw[:, 1], in_=k_v[:, 1])
+        nc.sync.dma_start(out=v_raw[:, 0], in_=v_v[:, 0])
         nc.sync.dma_start(out=v_raw[:, 1], in_=v_v[:, 1])
-        for h in range(8, H):
-            nc.sync.dma_start(out=q_raw[:, h], in_=q_v[:, h])
+        nc.sync.dma_start(out=mask_sb[:, 1, :], in_=m_v[:, 1, :])
+        nc.sync.dma_start(out=q_raw[:, :, 1, :], in_=q_v[:, :, 1, :])
+        for t in range(2, NT, 2):
+            nc.sync.dma_start(out=mask_sb[:, t : t + 2, :], in_=m_v[:, t : t + 2, :])
+            nc.sync.dma_start(out=q_raw[:, :, t : t + 2, :], in_=q_v[:, :, t : t + 2, :])
 
         nc.gpsimd.tensor_copy(out=sink_f[:], in_=sink_bf[:])
         nc.gpsimd.tensor_scalar(
@@ -119,14 +121,9 @@ def tile_deepseekv4attention_kernel(tc, query, key, value, attention_mask, sinks
             )
 
         def prep_qt_pe(b, q_ps):
-            hq, tp = divmod(b, 4)
-            for t2 in range(2):
-                for j in range(4):
-                    nc.tensor.transpose(
-                        out=q_ps[:, t2 * 4 + j, :],
-                        in_=q_raw[:, 4 * hq + j, 2 * tp + t2, :],
-                        identity=ident[:],
-                    )
+            t, octet = divmod(b, 2)
+            for j in range(8):
+                nc.tensor.transpose(out=q_ps[:, j, :], in_=q_raw[:, 8 * octet + j, t, :], identity=ident[:])
             x_ps["q%d" % b] = q_ps[:]
 
         def prep_qt_copy(b, on_vector=False):
@@ -141,6 +138,7 @@ def tile_deepseekv4attention_kernel(tc, query, key, value, attention_mask, sinks
         nmax = {}
         negm = {}
         den = {}
+        sdiff = {}
         dsum = {}
         rden = {}
         e_sb = {}
@@ -152,8 +150,8 @@ def tile_deepseekv4attention_kernel(tc, query, key, value, attention_mask, sinks
         o_sb = {}
 
         def where(i):
-            hq, r = divmod(i, 4 * NT)
-            t, j = divmod(r, 4)
+            t, r = divmod(i, H)
+            hq, j = divmod(r, 4)
             return hq, t, j
 
         def qk(i):
@@ -221,14 +219,19 @@ def tile_deepseekv4attention_kernel(tc, query, key, value, attention_mask, sinks
                 )
             e_sb[i] = e_t
 
-        def sink_term(quad):
+        def sink_diff(quad):
             hq, t, jz = where(4 * quad)
             d_t = small.tile([P, 4], F32, tag="sdiff")
+            nc.gpsimd.tensor_tensor(out=d_t[:], in0=negm[quad][:], in1=sink_f[:, 4 * hq : 4 * hq + 4], op=ALU.add)
+            sdiff[quad] = d_t
+
+        def sink_exp(quad):
+            nc.scalar.activation(out=den[quad][:, :, 2], in_=sdiff[quad][:], func=ACT.Exp)
+
+        def den_sum(quad):
             sum_t = small.tile([P, 4], F32, tag="esum")
             dsum_t = small.tile([P, 4], F32, tag="dsum")
-            nc.gpsimd.tensor_tensor(out=d_t[:], in0=negm[quad][:], in1=sink_f[:, 4 * hq : 4 * hq + 4], op=ALU.add)
             nc.gpsimd.tensor_tensor(out=sum_t[:], in0=den[quad][:, :, 0], in1=den[quad][:, :, 1], op=ALU.add)
-            nc.scalar.activation(out=den[quad][:, :, 2], in_=d_t[:], func=ACT.Exp)
             nc.gpsimd.tensor_tensor(out=dsum_t[:], in0=sum_t[:], in1=den[quad][:, :, 2], op=ALU.add)
             dsum[quad] = dsum_t
 
@@ -247,7 +250,7 @@ def tile_deepseekv4attention_kernel(tc, query, key, value, attention_mask, sinks
             et32 = et_sb[i // 4][:].rearrange("p c q t -> p (c q t)").bitcast(F32)
             dst = et32[:, 4 * P * j : 4 * P * (j + 1)].rearrange("p (c q u) -> p c q u", c=2, u=2)
             src = tr_ps[i][:].rearrange("p (c u) q -> p c q u", u=2)
-            if j in V_COPIES:
+            if copy_on_vector(i):
                 nc.vector.tensor_copy(out=dst, in_=src)
             else:
                 nc.scalar.copy(out=dst, in_=src)
@@ -316,10 +319,12 @@ def tile_deepseekv4attention_kernel(tc, query, key, value, attention_mask, sinks
         prep_mask_copy(0, 0, 4)
         prep_mask_copy(0, 4, 8, on_vector=True)
 
-        prep_at = {-1: ("m", 1), 1: ("q", 1), 2: ("m", 2), 4: ("m", 3), 5: ("q", 2)}
-        prep_at.update({9: ("m", 4), 13: ("q", 3), 17: ("m", 5), 21: ("m", 6), 25: ("m", 7), 33: ("k", 1)})
-        for b in range(4, NU // 8):
+        prep_at = {0: ("q", 1), 2: ("k", 1)}
+        for b in range(2, NU // 8):
             prep_at[8 * b - 3] = ("q", b)
+        for t in range(1, NT):
+            for half in range(2):
+                prep_at[16 * t - 15 + 8 * half] = ("m", (t, half))
 
         def quad_at(i, lag):
             last = i - lag
@@ -328,12 +333,22 @@ def tile_deepseekv4attention_kernel(tc, query, key, value, attention_mask, sinks
             return None
 
         for i in range(-1, NU + 3):
+            q_d = quad_at(i, 1)
             q_s = quad_at(i, 2)
+            q_m = quad_at(i, 3)
             q_r = quad_at(i, 4)
             q_mx1 = quad_at(i, 5)
             q_out = quad_at(i, 6)
-            if 0 <= i - 3 < NU:
+            if 0 <= i - 3 < NU and not copy_on_vector(i - 3):
                 p4(i - 3)
+            if i - 1 in prep_at:
+                kind, b = prep_at[i - 1]
+                if kind == "m":
+                    prep_mask_copy(b[0], 4 * b[1], 4 * b[1] + 4)
+                elif kind == "q":
+                    prep_qt_copy(b)
+                else:
+                    prep_kt_copy(b)
             if q_out is not None:
                 p6(q_out)
             if 0 <= i - 4 < NU:
@@ -342,43 +357,41 @@ def tile_deepseekv4attention_kernel(tc, query, key, value, attention_mask, sinks
                 rmax(i, 0)
                 rmax(i, 1)
                 tn(i)
+            if 0 <= i - 3 < NU and copy_on_vector(i - 3):
+                p4(i - 3)
             if q_r is not None:
                 recip(q_r)
-            if i in (3, 46):
+            if i in (3, 5):
                 prep_v(0 if i == 3 else 1)
-            if q_r is not None:
-                mx(q_r, 0, 2)
             if q_mx1 is not None:
-                mx(q_mx1, 2, 4)
+                mx(q_mx1)
             if i + 1 < NU:
                 qk(i + 1)
             if 0 <= i - 2 < NU:
                 tr(i - 2)
             if 0 <= i - 1 < NU:
                 ex(i - 1)
+            if q_d is not None:
+                sink_diff(q_d)
             if q_s is not None:
-                sink_term(q_s)
+                sink_exp(q_s)
+            if q_m is not None:
+                den_sum(q_m)
             if i == NU + 1:
-                sink_term(NQ - 1)
+                sink_diff(NQ - 1)
+                sink_exp(NQ - 1)
+                den_sum(NQ - 1)
             if i == NU + 2:
                 recip(NQ - 1)
                 mx(NQ - 1, 0, 3)
                 quantise(NU - 1)
                 mx(NQ - 1, 3, 4)
                 p6(NQ - 1)
-            if i - 1 in prep_at:
-                kind, b = prep_at[i - 1]
-                if kind == "m":
-                    prep_mask_copy(b)
-                elif kind == "q":
-                    prep_qt_copy(b)
-                else:
-                    prep_kt_copy(b)
             if i in prep_at:
                 kind, b = prep_at[i]
                 prep_ps = ps_x.tile([P, 8, P], BF16, tag="x")
                 if kind == "m":
-                    prep_mask_pe(b, prep_ps)
+                    prep_mask_pe(b[0], prep_ps, 4 * b[1], 4 * b[1] + 4)
                 elif kind == "q":
                     prep_qt_pe(b, prep_ps)
                 else:

@@ -27,7 +27,7 @@ FLOPS = 2 * 2 * H * S * S * D
 
 
 def copy_on_vector(i):
-    return i % 4 == 3
+    return i % 4 == 3 or i == NU - 2
 
 
 def tile_deepseekv4attention_kernel(tc, query, key, value, attention_mask, sinks, out):
@@ -70,7 +70,8 @@ def tile_deepseekv4attention_kernel(tc, query, key, value, attention_mask, sinks
         make_identity(nc, ident32[:])
 
         nc.scalar.dma_start(out=sink_bf[:], in_=sinks.partition_broadcast(P))
-        nc.sync.dma_start(out=k_raw[:, 0], in_=k_v[:, 0])
+        nc.sync.dma_start(out=k_raw[:, 0, 0:4], in_=k_v[:, 0, 0:4])
+        nc.sync.dma_start(out=k_raw[:, 0, 4:8], in_=k_v[:, 0, 4:8])
         nc.sync.dma_start(out=q_raw[:, 0:8, 0, :], in_=q_v[:, 0:8, 0, :])
         nc.sync.dma_start(out=mask_sb[:, 0, :], in_=m_v[:, 0, :])
         nc.sync.dma_start(out=q_raw[:, 8:16, 0, :], in_=q_v[:, 8:16, 0, :])
@@ -236,10 +237,14 @@ def tile_deepseekv4attention_kernel(tc, query, key, value, attention_mask, sinks
             dsum[quad] = dsum_t
 
         def tr(i):
-            tr_t = ps_t.tile([P, 4, P], F32, tag="tr")
+            if i < NU - 2:
+                tr_t = ps_t.tile([P, 4, P], F32, tag="tr")
+            else:
+                tr_t = ps_s.tile([P, 4, P], F32, tag="sc")
             words = e_sb[i][:].bitcast(F32)
             for a in range(4):
-                nc.tensor.transpose(out=tr_t[:, a, :], in_=words[:, P * a : P * a + P], identity=ident32[:])
+                c, u = divmod(a, 2)
+                nc.tensor.transpose(out=tr_t[:, 2 * u + c, :], in_=words[:, P * a : P * a + P], identity=ident32[:])
             tr_ps[i] = tr_t
 
         def p4(i):
@@ -248,8 +253,8 @@ def tile_deepseekv4attention_kernel(tc, query, key, value, attention_mask, sinks
                 et_t = et_pool.tile([P, 8, P, 4], BF16, tag="et", align_bytes=64)
                 et_sb[i // 4] = et_t
             et32 = et_sb[i // 4][:].rearrange("p c q t -> p (c q t)").bitcast(F32)
-            dst = et32[:, 4 * P * j : 4 * P * (j + 1)].rearrange("p (c q u) -> p c q u", c=2, u=2)
-            src = tr_ps[i][:].rearrange("p (c u) q -> p c q u", u=2)
+            dst = et32[:, 4 * P * j : 4 * P * (j + 1)].rearrange("p (g w u) -> p g u w", w=4, u=2)
+            src = tr_ps[i][:].rearrange("p (u c) q -> p u (c q)", u=2).rearrange("p u (g w) -> p g u w", w=4)
             if copy_on_vector(i):
                 nc.vector.tensor_copy(out=dst, in_=src)
             else:
@@ -310,8 +315,17 @@ def tile_deepseekv4attention_kernel(tc, query, key, value, attention_mask, sinks
             nc.sync.dma_start(out=o_v[:, t, 4 * hq + j0 : 4 * hq + j1, :], in_=o_t[:, j0:j1, :])
 
         head_ps = [ps_s.tile([P, 8, P], BF16, tag="sc", name="head_ps") for n in range(4)]
+        warm_ps = ps_x.tile([P, P], F32, tag="x")
+
+        def warm(n):
+            for k in range(n):
+                nc.tensor.matmul(out=warm_ps[:], lhsT=ident[:], rhs=ident[:], start=True, stop=True)
+
+        warm(14)
         prep_kt_pe(0, head_ps[0])
+        warm(8)
         prep_qt_pe(0, head_ps[1])
+        warm(8)
         prep_mask_pe(0, head_ps[2], 0, 4)
         prep_mask_pe(0, head_ps[3], 4, 8)
         prep_kt_copy(0)
@@ -319,7 +333,7 @@ def tile_deepseekv4attention_kernel(tc, query, key, value, attention_mask, sinks
         prep_mask_copy(0, 0, 4)
         prep_mask_copy(0, 4, 8, on_vector=True)
 
-        prep_at = {0: ("q", 1), 2: ("k", 1)}
+        prep_at = {0: ("k", 1), 3: ("q", 1)}
         for b in range(2, NU // 8):
             prep_at[8 * b - 3] = ("q", b)
         for t in range(1, NT):
@@ -351,7 +365,7 @@ def tile_deepseekv4attention_kernel(tc, query, key, value, attention_mask, sinks
                     prep_kt_copy(b)
             if q_out is not None:
                 p6(q_out)
-            if 0 <= i - 4 < NU:
+            if 0 <= i - 4 < NU - 2:
                 quantise(i - 4)
             if 0 <= i < NU:
                 rmax(i, 0)
@@ -359,6 +373,8 @@ def tile_deepseekv4attention_kernel(tc, query, key, value, attention_mask, sinks
                 tn(i)
             if 0 <= i - 3 < NU and copy_on_vector(i - 3):
                 p4(i - 3)
+            if i == NU + 1:
+                quantise(NU - 2)
             if q_r is not None:
                 recip(q_r)
             if i in (3, 5):
@@ -377,15 +393,15 @@ def tile_deepseekv4attention_kernel(tc, query, key, value, attention_mask, sinks
                 sink_exp(q_s)
             if q_m is not None:
                 den_sum(q_m)
-            if i == NU + 1:
+            if i == NU:
                 sink_diff(NQ - 1)
                 sink_exp(NQ - 1)
                 den_sum(NQ - 1)
             if i == NU + 2:
-                recip(NQ - 1)
                 mx(NQ - 1, 0, 3)
                 quantise(NU - 1)
                 mx(NQ - 1, 3, 4)
+                recip(NQ - 1)
                 p6(NQ - 1)
             if i in prep_at:
                 kind, b = prep_at[i]

@@ -253,8 +253,8 @@ def tile_deepseekv4attention_kernel(tc, query, key, value, attention_mask, sinks
                 et_t = et_pool.tile([P, 8, P, 4], BF16, tag="et", align_bytes=64)
                 et_sb[i // 4] = et_t
             et32 = et_sb[i // 4][:].rearrange("p c q t -> p (c q t)").bitcast(F32)
-            dst = et32[:, 4 * P * j : 4 * P * (j + 1)].rearrange("p (g w u) -> p g u w", w=4, u=2)
-            src = tr_ps[i][:].rearrange("p (u c) q -> p u (c q)", u=2).rearrange("p u (g w) -> p g u w", w=4)
+            dst = et32[:, 4 * P * j : 4 * P * (j + 1)].rearrange("p (n u) -> p n u", u=2)
+            src = tr_ps[i][:].rearrange("p (u c) q -> p (c q) u", u=2)
             if copy_on_vector(i):
                 nc.vector.tensor_copy(out=dst, in_=src)
             else:
@@ -346,6 +346,20 @@ def tile_deepseekv4attention_kernel(tc, query, key, value, attention_mask, sinks
                 return last // 4
             return None
 
+        def prep_copy(i, late):
+            if i - 1 not in prep_at:
+                return
+            kind, b = prep_at[i - 1]
+            on_vector = i > 8 and (kind == "q")
+            if on_vector != late:
+                return
+            if kind == "m":
+                prep_mask_copy(b[0], 4 * b[1], 4 * b[1] + 4, on_vector=on_vector)
+            elif kind == "q":
+                prep_qt_copy(b, on_vector=on_vector)
+            else:
+                prep_kt_copy(b)
+
         for i in range(-1, NU + 3):
             q_d = quad_at(i, 1)
             q_s = quad_at(i, 2)
@@ -355,14 +369,7 @@ def tile_deepseekv4attention_kernel(tc, query, key, value, attention_mask, sinks
             q_out = quad_at(i, 6)
             if 0 <= i - 3 < NU and not copy_on_vector(i - 3):
                 p4(i - 3)
-            if i - 1 in prep_at:
-                kind, b = prep_at[i - 1]
-                if kind == "m":
-                    prep_mask_copy(b[0], 4 * b[1], 4 * b[1] + 4)
-                elif kind == "q":
-                    prep_qt_copy(b)
-                else:
-                    prep_kt_copy(b)
+            prep_copy(i, False)
             if q_out is not None:
                 p6(q_out)
             if 0 <= i - 4 < NU - 2:
@@ -375,6 +382,7 @@ def tile_deepseekv4attention_kernel(tc, query, key, value, attention_mask, sinks
                 p4(i - 3)
             if i == NU + 1:
                 quantise(NU - 2)
+            prep_copy(i, True)
             if q_r is not None:
                 recip(q_r)
             if i in (3, 5):
@@ -399,10 +407,11 @@ def tile_deepseekv4attention_kernel(tc, query, key, value, attention_mask, sinks
                 den_sum(NQ - 1)
             if i == NU + 2:
                 mx(NQ - 1, 0, 3)
+                recip(NQ - 1)
+                p6(NQ - 1, 0, 3)
                 quantise(NU - 1)
                 mx(NQ - 1, 3, 4)
-                recip(NQ - 1)
-                p6(NQ - 1)
+                p6(NQ - 1, 3, 4)
             if i in prep_at:
                 kind, b = prep_at[i]
                 prep_ps = ps_x.tile([P, 8, P], BF16, tag="x")

@@ -260,18 +260,19 @@ def tile_deepseekv4attention_kernel(tc, query, key, value, attention_mask, sinks
             else:
                 nc.scalar.copy(out=dst, in_=src)
 
-        def quantise(i):
+        def quantise(i, n=2):
             quad, j = divmod(i, 4)
+            j = j + 1 - n
             if j == 0:
                 c_t = c_pool.tile([P, 8 * P], U32, tag="codes", align_bytes=64)
                 sc_b = c_pool.tile([P, 8 * P], U8, tag="scales", align_bytes=64)
                 codes[quad] = c_t
                 scales[quad] = sc_b
-            cols = slice(2 * P * j, 2 * P * (j + 1))
+            cols = slice(2 * P * j, 2 * P * (j + n))
             nc.vector.quantize_mx(
                 out=codes[quad][:, cols].bitcast(FP8X4),
                 scales=scales[quad][:, cols],
-                in_=et_sb[quad][:, 2 * j : 2 * j + 2].rearrange("p c q t -> p (c q t)"),
+                in_=et_sb[quad][:, 2 * j : 2 * j + 2 * n].rearrange("p c q t -> p (c q t)"),
             )
 
         def mx(quad, j0=0, j1=4):
@@ -372,7 +373,7 @@ def tile_deepseekv4attention_kernel(tc, query, key, value, attention_mask, sinks
             prep_copy(i, False)
             if q_out is not None:
                 p6(q_out)
-            if 0 <= i - 4 < NU - 2:
+            if 0 <= i - 4 < NU - 2 and i % 2 == 1:
                 quantise(i - 4)
             if 0 <= i < NU:
                 rmax(i, 0)
@@ -381,7 +382,7 @@ def tile_deepseekv4attention_kernel(tc, query, key, value, attention_mask, sinks
             if 0 <= i - 3 < NU and copy_on_vector(i - 3):
                 p4(i - 3)
             if i == NU + 1:
-                quantise(NU - 2)
+                quantise(NU - 2, 1)
             prep_copy(i, True)
             if q_r is not None:
                 recip(q_r)
@@ -409,7 +410,7 @@ def tile_deepseekv4attention_kernel(tc, query, key, value, attention_mask, sinks
                 mx(NQ - 1, 0, 3)
                 recip(NQ - 1)
                 p6(NQ - 1, 0, 3)
-                quantise(NU - 1)
+                quantise(NU - 1, 1)
                 mx(NQ - 1, 3, 4)
                 p6(NQ - 1, 3, 4)
             if i in prep_at:

@@ -27,7 +27,7 @@ FLOPS = 2 * 2 * H * S * S * D
 
 
 def copy_on_vector(i):
-    return i % 4 == 3 or i == NU - 2
+    return i == NU - 2 or (i % 4 == 3 and i < NU - 1)
 
 
 def tile_deepseekv4attention_kernel(tc, query, key, value, attention_mask, sinks, out):
@@ -72,10 +72,12 @@ def tile_deepseekv4attention_kernel(tc, query, key, value, attention_mask, sinks
         nc.scalar.dma_start(out=sink_bf[:], in_=sinks.partition_broadcast(P))
         nc.sync.dma_start(out=k_raw[:, 0, 0:4], in_=k_v[:, 0, 0:4])
         nc.sync.dma_start(out=k_raw[:, 0, 4:8], in_=k_v[:, 0, 4:8])
-        nc.sync.dma_start(out=q_raw[:, 0:8, 0, :], in_=q_v[:, 0:8, 0, :])
-        nc.sync.dma_start(out=mask_sb[:, 0, :], in_=m_v[:, 0, :])
-        nc.sync.dma_start(out=q_raw[:, 8:16, 0, :], in_=q_v[:, 8:16, 0, :])
+        nc.sync.dma_start(out=q_raw[:, 0:4, 0, :], in_=q_v[:, 0:4, 0, :])
+        nc.sync.dma_start(out=mask_sb[:, 0, 0:HALF], in_=m_v[:, 0, 0:HALF])
+        nc.sync.dma_start(out=mask_sb[:, 0, HALF:S], in_=m_v[:, 0, HALF:S])
+        nc.sync.dma_start(out=q_raw[:, 4:8, 0, :], in_=q_v[:, 4:8, 0, :])
         nc.sync.dma_start(out=k_raw[:, 1], in_=k_v[:, 1])
+        nc.sync.dma_start(out=q_raw[:, 8:16, 0, :], in_=q_v[:, 8:16, 0, :])
         nc.sync.dma_start(out=v_raw[:, 0], in_=v_v[:, 0])
         nc.sync.dma_start(out=v_raw[:, 1], in_=v_v[:, 1])
         nc.sync.dma_start(out=mask_sb[:, 1, :], in_=m_v[:, 1, :])
@@ -121,22 +123,25 @@ def tile_deepseekv4attention_kernel(tc, query, key, value, attention_mask, sinks
                 in_=v_grouped[:].rearrange("p c d t -> p (c d t)"),
             )
 
-        def prep_qt_pe(b, q_ps):
+        def prep_qt_pe(b, q_ps, j0=0, j1=8):
             t, octet = divmod(b, 2)
-            for j in range(8):
+            for j in range(j0, j1):
                 nc.tensor.transpose(out=q_ps[:, j, :], in_=q_raw[:, 8 * octet + j, t, :], identity=ident[:])
             x_ps["q%d" % b] = q_ps[:]
 
-        def prep_qt_copy(b, on_vector=False):
-            qt = qt_pool.tile([P, 8, P], BF16, tag="qtsb")
+        def prep_qt_copy(b, on_vector=False, j0=0, j1=8):
+            if j0 == 0:
+                qt = qt_pool.tile([P, 8, P], BF16, tag="qtsb")
+                qt_sb[b] = qt
+            dst, src = qt_sb[b][:, j0:j1, :], x_ps["q%d" % b][:, j0:j1, :]
             if on_vector:
-                nc.vector.tensor_copy(out=qt[:], in_=x_ps["q%d" % b])
+                nc.vector.tensor_copy(out=dst, in_=src)
             else:
-                nc.scalar.copy(out=qt[:], in_=x_ps["q%d" % b])
-            qt_sb[b] = qt
+                nc.scalar.copy(out=dst, in_=src)
 
         sc = {}
         nmax = {}
+        ncap = {}
         negm = {}
         den = {}
         sdiff = {}
@@ -184,23 +189,20 @@ def tile_deepseekv4attention_kernel(tc, query, key, value, attention_mask, sinks
             nc.vector.tensor_reduce(out=n_t[:], in_=sc[i, c][:], axis=AX.X, op=ALU.max, negate=True)
             nmax[i, c] = n_t
 
-        def tn(i):
+        def tn(i, c):
             hq, t, j = where(i)
             h = 4 * hq + j
-            if j == 0:
-                n4_t = small.tile([P, 4], F32, tag="negm")
-                negm[i // 4] = n4_t
-            t_t = small.tile([P, 1], F32, tag="tmp")
+            if c == 0:
+                if j == 0:
+                    n4_t = small.tile([P, 4], F32, tag="negm")
+                    negm[i // 4] = n4_t
+                t_t = small.tile([P, 1], F32, tag="tmp")
+                ncap[i] = t_t
+                out, cap = t_t[:], nsink[:, h : h + 1]
+            else:
+                out, cap = negm[i // 4][:, j : j + 1], ncap[i][:]
             nc.gpsimd.tensor_scalar(
-                out=t_t[:], in0=nmax[i, 0][:], scalar1=nmax[i, 1][:], scalar2=SCALE, op0=ALU.min, op1=ALU.mult
-            )
-            nc.gpsimd.tensor_scalar(
-                out=negm[i // 4][:, j : j + 1],
-                in0=t_t[:],
-                scalar1=nsink[:, h : h + 1],
-                scalar2=0.0,
-                op0=ALU.min,
-                op1=ALU.add,
+                out=out, in0=nmax[i, c][:], scalar1=SCALE, scalar2=cap, op0=ALU.mult, op1=ALU.min
             )
 
         def ex(i):
@@ -278,8 +280,9 @@ def tile_deepseekv4attention_kernel(tc, query, key, value, attention_mask, sinks
         def mx(quad, j0=0, j1=4):
             if j0 == 0:
                 pv_t = ps_x.tile([P, 4, D], F32, tag="x")
-                pv[quad] = pv_t
-            pv_t = pv[quad]
+            else:
+                pv_t = ps_s.tile([P, 4, D], F32, tag="sc")
+            pv[quad] = pv_t
             hq = where(4 * quad)[0]
             for j in range(j0, j1):
                 g = (4 * hq + j) // (H // HKV)
@@ -322,17 +325,18 @@ def tile_deepseekv4attention_kernel(tc, query, key, value, attention_mask, sinks
             for k in range(n):
                 nc.tensor.matmul(out=warm_ps[:], lhsT=ident[:], rhs=ident[:], start=True, stop=True)
 
-        warm(14)
+        warm(30)
         prep_kt_pe(0, head_ps[0])
-        warm(8)
-        prep_qt_pe(0, head_ps[1])
-        warm(8)
+        prep_qt_pe(0, head_ps[1], 0, 4)
+        prep_kt_copy(0)
+        prep_qt_copy(0, True, 0, 4)
         prep_mask_pe(0, head_ps[2], 0, 4)
         prep_mask_pe(0, head_ps[3], 4, 8)
-        prep_kt_copy(0)
-        prep_qt_copy(0, on_vector=True)
         prep_mask_copy(0, 0, 4)
         prep_mask_copy(0, 4, 8, on_vector=True)
+        rest_ps = ps_x.tile([P, 8, P], BF16, tag="x")
+        prep_qt_pe(0, rest_ps, 4, 8)
+        prep_qt_copy(0, True, 4, 8)
 
         prep_at = {0: ("k", 1), 3: ("q", 1)}
         for b in range(2, NU // 8):
@@ -347,17 +351,14 @@ def tile_deepseekv4attention_kernel(tc, query, key, value, attention_mask, sinks
                 return last // 4
             return None
 
-        def prep_copy(i, late):
+        def prep_copy(i):
             if i - 1 not in prep_at:
                 return
             kind, b = prep_at[i - 1]
-            on_vector = i > 8 and (kind == "q")
-            if on_vector != late:
-                return
             if kind == "m":
-                prep_mask_copy(b[0], 4 * b[1], 4 * b[1] + 4, on_vector=on_vector)
+                prep_mask_copy(b[0], 4 * b[1], 4 * b[1] + 4)
             elif kind == "q":
-                prep_qt_copy(b, on_vector=on_vector)
+                prep_qt_copy(b, on_vector=(i > 8))
             else:
                 prep_kt_copy(b)
 
@@ -370,20 +371,19 @@ def tile_deepseekv4attention_kernel(tc, query, key, value, attention_mask, sinks
             q_out = quad_at(i, 6)
             if 0 <= i - 3 < NU and not copy_on_vector(i - 3):
                 p4(i - 3)
-            prep_copy(i, False)
             if q_out is not None:
                 p6(q_out)
             if 0 <= i - 4 < NU - 2 and i % 2 == 1:
                 quantise(i - 4)
             if 0 <= i < NU:
                 rmax(i, 0)
+                tn(i, 0)
                 rmax(i, 1)
-                tn(i)
+                tn(i, 1)
             if 0 <= i - 3 < NU and copy_on_vector(i - 3):
                 p4(i - 3)
             if i == NU + 1:
                 quantise(NU - 2, 1)
-            prep_copy(i, True)
             if q_r is not None:
                 recip(q_r)
             if i in (3, 5):
@@ -396,6 +396,7 @@ def tile_deepseekv4attention_kernel(tc, query, key, value, attention_mask, sinks
                 tr(i - 2)
             if 0 <= i - 1 < NU:
                 ex(i - 1)
+            prep_copy(i)
             if q_d is not None:
                 sink_diff(q_d)
             if q_s is not None:
@@ -409,8 +410,8 @@ def tile_deepseekv4attention_kernel(tc, query, key, value, attention_mask, sinks
             if i == NU + 2:
                 mx(NQ - 1, 0, 3)
                 recip(NQ - 1)
-                p6(NQ - 1, 0, 3)
                 quantise(NU - 1, 1)
+                p6(NQ - 1, 0, 3)
                 mx(NQ - 1, 3, 4)
                 p6(NQ - 1, 3, 4)
             if i in prep_at:

@@ -325,7 +325,7 @@ def tile_deepseekv4attention_kernel(tc, query, key, value, attention_mask, sinks
             for k in range(n):
                 nc.tensor.matmul(out=warm_ps[:], lhsT=ident[:], rhs=ident[:], start=True, stop=True)
 
-        warm(30)
+        warm(18)
         prep_kt_pe(0, head_ps[0])
         prep_qt_pe(0, head_ps[1], 0, 4)
         prep_kt_copy(0)

@@ -47,14 +47,14 @@ def tile_deepseekv4attention_kernel(tc, query, key, value, attention_mask, sinks
 
         q_v = query[0].rearrange("h (p t) d -> p h t d", t=NT)
         m_v = attention_mask[0, 0].rearrange("(p t) k -> p t k", t=NT)
-        k_v = key[0].rearrange("g (a p) d -> p g a d", p=P)
-        v_v = value[0].rearrange("g (a p e) d -> p g a e d", p=P, e=2)
+        k_v = key[0].rearrange("g (a n e) d -> n g a e d", n=P, e=2)
+        v_v = value[0].rearrange("g (a n z e) d -> e n g a z d", n=P // 2, z=2, e=2)
         o_v = out[0].rearrange("(p t) h d -> p t h d", t=NT)
 
         q_raw = const.tile([P, H, NT, D], BF16)
         mask_sb = const.tile([P, NT, S], BF16)
         mask_t = const.tile([P, NT, 8, P], F32)
-        k_raw = const.tile([P, HKV, NT, D], BF16)
+        k_raw = const.tile([P, HKV, 4, 2, D], BF16)
         v_raw = const.tile([P, HKV, 4, 2, D], BF16)
         sink_bf = const.tile([P, H], BF16)
         sink_f = const.tile([P, H], F32)
@@ -70,17 +70,20 @@ def tile_deepseekv4attention_kernel(tc, query, key, value, attention_mask, sinks
         make_identity(nc, ident32[:])
 
         nc.scalar.dma_start(out=sink_bf[:], in_=sinks.partition_broadcast(P))
-        nc.sync.dma_start(out=k_raw[:, 0, 0:4], in_=k_v[:, 0, 0:4])
-        nc.sync.dma_start(out=k_raw[:, 0, 4:8], in_=k_v[:, 0, 4:8])
+        nc.sync.dma_start(out=k_raw[:, 0, 0:2], in_=k_v[:, 0, 0:2])
+        nc.sync.dma_start(out=k_raw[:, 0, 2:4], in_=k_v[:, 0, 2:4])
         nc.sync.dma_start(out=q_raw[:, 0:4, 0, :], in_=q_v[:, 0:4, 0, :])
         nc.sync.dma_start(out=mask_sb[:, 0, 0:HALF], in_=m_v[:, 0, 0:HALF])
         nc.sync.dma_start(out=mask_sb[:, 0, HALF:S], in_=m_v[:, 0, HALF:S])
         nc.sync.dma_start(out=q_raw[:, 4:8, 0, :], in_=q_v[:, 4:8, 0, :])
         nc.sync.dma_start(out=k_raw[:, 1], in_=k_v[:, 1])
         nc.sync.dma_start(out=q_raw[:, 8:16, 0, :], in_=q_v[:, 8:16, 0, :])
-        nc.sync.dma_start(out=v_raw[:, 0], in_=v_v[:, 0])
-        nc.sync.dma_start(out=v_raw[:, 1], in_=v_v[:, 1])
         nc.sync.dma_start(out=mask_sb[:, 1, :], in_=m_v[:, 1, :])
+        for g in range(HKV):
+            for a in range(4):
+                for e in range(2):
+                    half = slice(P // 2 * e, P // 2 * e + P // 2)
+                    nc.sync.dma_start(out=v_raw[half, g, a], in_=v_v[e, :, g, a])
         nc.sync.dma_start(out=q_raw[:, :, 1, :], in_=q_v[:, :, 1, :])
         for t in range(2, NT, 2):
             nc.sync.dma_start(out=mask_sb[:, t : t + 2, :], in_=m_v[:, t : t + 2, :])
@@ -96,20 +99,22 @@ def tile_deepseekv4attention_kernel(tc, query, key, value, attention_mask, sinks
 
         def prep_kt_pe(g, kt_ps):
             for a in range(NT):
-                nc.tensor.transpose(out=kt_ps[:, a, :], in_=k_raw[:, g, a, :], identity=ident[:])
+                nc.tensor.transpose(out=kt_ps[:, a, :], in_=k_raw[:, g, a // 2, a % 2, :], identity=ident[:])
             x_ps["k%d" % g] = kt_ps[:]
 
         def prep_kt_copy(g):
             nc.scalar.copy(out=kt_sb[:, g, :], in_=x_ps["k%d" % g].rearrange("p a k -> p (a k)"))
 
-        def prep_mask_pe(t, mp, a0=0, a1=8):
-            for a in range(a0, a1):
-                nc.tensor.transpose(out=mp[:, a - a0, :], in_=mask_sb[:, t, P * a : P * a + P], identity=ident[:])
-            x_ps["m%d_%d" % (t, a0)] = mp[:, 0 : a1 - a0, :]
+        def prep_mask_pe(t, mp, w0, w1):
+            pairs = mask_sb[:, t, :].bitcast(F32)
+            for w in range(w0, w1):
+                nc.tensor.transpose(out=mp[:, w - w0, :], in_=pairs[:, P * w : P * w + P], identity=ident32[:])
+            x_ps["m%d_%d" % (t, w0)] = mp[:, 0 : w1 - w0, :]
 
-        def prep_mask_copy(t, a0=0, a1=8, on_vector=False):
-            src = x_ps["m%d_%d" % (t, a0)]
-            dst = mask_t[:, t, a0:a1, :]
+        def prep_mask_copy(t, w0, w1, on_vector=False):
+            pairs = x_ps["m%d_%d" % (t, w0)].rearrange("p w q -> p (w q)").bitcast(BF16)
+            src = pairs.rearrange("p (w q e) -> p w e q", w=w1 - w0, e=2)
+            dst = mask_t[:, t, 2 * w0 : 2 * w1, :].rearrange("p (w e) q -> p w e q", e=2)
             if on_vector:
                 nc.vector.tensor_scalar(out=dst, in0=src, scalar1=RSCALE, scalar2=None, op0=ALU.mult)
             else:
@@ -318,7 +323,8 @@ def tile_deepseekv4attention_kernel(tc, query, key, value, attention_mask, sinks
             )
             nc.sync.dma_start(out=o_v[:, t, 4 * hq + j0 : 4 * hq + j1, :], in_=o_t[:, j0:j1, :])
 
-        head_ps = [ps_s.tile([P, 8, P], BF16, tag="sc", name="head_ps") for n in range(4)]
+        head_ps = [ps_s.tile([P, 8, P], BF16, tag="sc", name="head_ps") for n in range(2)]
+        mask_ps = [ps_s.tile([P, 4, P], F32, tag="sc", name="mask_ps") for n in range(2)]
         warm_ps = ps_x.tile([P, P], F32, tag="x")
 
         def warm(n):
@@ -330,10 +336,10 @@ def tile_deepseekv4attention_kernel(tc, query, key, value, attention_mask, sinks
         prep_qt_pe(0, head_ps[1], 0, 4)
         prep_kt_copy(0)
         prep_qt_copy(0, True, 0, 4)
-        prep_mask_pe(0, head_ps[2], 0, 4)
-        prep_mask_pe(0, head_ps[3], 4, 8)
-        prep_mask_copy(0, 0, 4)
-        prep_mask_copy(0, 4, 8, on_vector=True)
+        prep_mask_pe(0, mask_ps[0], 0, 2)
+        prep_mask_pe(0, mask_ps[1], 2, 4)
+        prep_mask_copy(0, 0, 2)
+        prep_mask_copy(0, 2, 4, on_vector=True)
         rest_ps = ps_x.tile([P, 8, P], BF16, tag="x")
         prep_qt_pe(0, rest_ps, 4, 8)
         prep_qt_copy(0, True, 4, 8)
@@ -356,7 +362,7 @@ def tile_deepseekv4attention_kernel(tc, query, key, value, attention_mask, sinks
                 return
             kind, b = prep_at[i - 1]
             if kind == "m":
-                prep_mask_copy(b[0], 4 * b[1], 4 * b[1] + 4)
+                prep_mask_copy(b[0], 2 * b[1], 2 * b[1] + 2)
             elif kind == "q":
                 prep_qt_copy(b, on_vector=(i > 8))
             else:
@@ -416,10 +422,12 @@ def tile_deepseekv4attention_kernel(tc, query, key, value, attention_mask, sinks
                 p6(NQ - 1, 3, 4)
             if i in prep_at:
                 kind, b = prep_at[i]
-                prep_ps = ps_x.tile([P, 8, P], BF16, tag="x")
                 if kind == "m":
-                    prep_mask_pe(b[0], prep_ps, 4 * b[1], 4 * b[1] + 4)
-                elif kind == "q":
+                    prep_ps = ps_x.tile([P, 4, P], F32, tag="x")
+                    prep_mask_pe(b[0], prep_ps, 2 * b[1], 2 * b[1] + 2)
+                    continue
+                prep_ps = ps_x.tile([P, 8, P], BF16, tag="x")
+                if kind == "q":
                     prep_qt_pe(b, prep_ps)
                 else:
                     prep_kt_pe(b, prep_ps)

@@ -131,14 +131,14 @@ def tile_deepseekv4attention_kernel(tc, query, key, value, attention_mask, sinks
         def prep_qt_pe(b, q_ps, j0=0, j1=8):
             t, octet = divmod(b, 2)
             for j in range(j0, j1):
-                nc.tensor.transpose(out=q_ps[:, j, :], in_=q_raw[:, 8 * octet + j, t, :], identity=ident[:])
-            x_ps["q%d" % b] = q_ps[:]
+                nc.tensor.transpose(out=q_ps[:, j % 4 if j1 - j0 == 4 else j, :], in_=q_raw[:, 8 * octet + j, t, :], identity=ident[:])
+            x_ps["q%d" % b] = q_ps
 
         def prep_qt_copy(b, on_vector=False, j0=0, j1=8):
             if j0 == 0:
                 qt = qt_pool.tile([P, 8, P], BF16, tag="qtsb")
                 qt_sb[b] = qt
-            dst, src = qt_sb[b][:, j0:j1, :], x_ps["q%d" % b][:, j0:j1, :]
+            dst, src = qt_sb[b][:, j0:j1, :], x_ps["q%d" % b][:, 0 : j1 - j0, :]
             if on_vector:
                 nc.vector.tensor_copy(out=dst, in_=src)
             else:
@@ -344,12 +344,9 @@ def tile_deepseekv4attention_kernel(tc, query, key, value, attention_mask, sinks
         prep_qt_pe(0, rest_ps, 4, 8)
         prep_qt_copy(0, True, 4, 8)
 
-        prep_at = {0: ("k", 1), 3: ("q", 1)}
-        for b in range(2, NU // 8):
-            prep_at[8 * b - 3] = ("q", b)
-        for t in range(1, NT):
-            for half in range(2):
-                prep_at[16 * t - 15 + 8 * half] = ("m", (t, half))
+        prep_at = {0: ("k", 1)}
+        for n in range(1, NQ - 1):
+            prep_at[4 * n - 3] = ("qm", n)
 
         def quad_at(i, lag):
             last = i - lag
@@ -360,13 +357,16 @@ def tile_deepseekv4attention_kernel(tc, query, key, value, attention_mask, sinks
         def prep_copy(i):
             if i - 1 not in prep_at:
                 return
-            kind, b = prep_at[i - 1]
-            if kind == "m":
-                prep_mask_copy(b[0], 2 * b[1], 2 * b[1] + 2)
-            elif kind == "q":
-                prep_qt_copy(b, on_vector=(i > 8))
-            else:
-                prep_kt_copy(b)
+            kind, n = prep_at[i - 1]
+            if kind == "k":
+                prep_kt_copy(n)
+                return
+            b, half = divmod(n + 1, 2)
+            if b < NU // 8:
+                prep_qt_copy(b, i > 8, 4 * half, 4 * half + 4)
+            t, w = divmod(n - 1, 4)
+            if t + 1 < NT:
+                prep_mask_copy(t + 1, w, w + 1)
 
         for i in range(-1, NU + 3):
             q_d = quad_at(i, 1)
@@ -392,7 +392,7 @@ def tile_deepseekv4attention_kernel(tc, query, key, value, attention_mask, sinks
                 quantise(NU - 2, 1)
             if q_r is not None:
                 recip(q_r)
-            if i in (3, 5):
+            if i in (3, 7):
                 prep_v(0 if i == 3 else 1)
             if q_mx1 is not None:
                 mx(q_mx1)
@@ -421,13 +421,15 @@ def tile_deepseekv4attention_kernel(tc, query, key, value, attention_mask, sinks
                 mx(NQ - 1, 3, 4)
                 p6(NQ - 1, 3, 4)
             if i in prep_at:
-                kind, b = prep_at[i]
-                if kind == "m":
-                    prep_ps = ps_x.tile([P, 4, P], F32, tag="x")
-                    prep_mask_pe(b[0], prep_ps, 2 * b[1], 2 * b[1] + 2)
-                    continue
-                prep_ps = ps_x.tile([P, 8, P], BF16, tag="x")
-                if kind == "q":
-                    prep_qt_pe(b, prep_ps)
+                kind, n = prep_at[i]
+                if kind == "k":
+                    prep_ps = ps_x.tile([P, 8, P], BF16, tag="x")
+                    prep_kt_pe(n, prep_ps)
                 else:
-                    prep_kt_pe(b, prep_ps)
+                    prep_ps = ps_x.tile([P, 4, P], F32, tag="x")
+                    b, half = divmod(n + 1, 2)
+                    if b < NU // 8:
+                        prep_qt_pe(b, prep_ps[:, 0:2].rearrange("p w q -> p (w q)").bitcast(BF16).rearrange("p (j q) -> p j q", q=P), 4 * half, 4 * half + 4)
+                    t, w = divmod(n - 1, 4)
+                    if t + 1 < NT:
+                        prep_mask_pe(t + 1, prep_ps[:, 2:4], w, w + 1)

@@ -69,12 +69,12 @@ def tile_deepseekv4attention_kernel(tc, query, key, value, attention_mask, sinks
         make_identity(nc, ident[:])
         make_identity(nc, ident32[:])
 
-        nc.scalar.dma_start(out=sink_bf[:], in_=sinks.partition_broadcast(P))
         nc.sync.dma_start(out=k_raw[:, 0, 0:2], in_=k_v[:, 0, 0:2])
         nc.sync.dma_start(out=k_raw[:, 0, 2:4], in_=k_v[:, 0, 2:4])
         nc.sync.dma_start(out=q_raw[:, 0:4, 0, :], in_=q_v[:, 0:4, 0, :])
         nc.sync.dma_start(out=mask_sb[:, 0, 0:HALF], in_=m_v[:, 0, 0:HALF])
         nc.sync.dma_start(out=mask_sb[:, 0, HALF:S], in_=m_v[:, 0, HALF:S])
+        nc.sync.dma_start(out=sink_bf[:], in_=sinks.partition_broadcast(P))
         nc.sync.dma_start(out=q_raw[:, 4:8, 0, :], in_=q_v[:, 4:8, 0, :])
         nc.sync.dma_start(out=k_raw[:, 1], in_=k_v[:, 1])
         nc.sync.dma_start(out=q_raw[:, 8:16, 0, :], in_=q_v[:, 8:16, 0, :])

from contextlib import ExitStack

import concourse.mybir as mybir
from concourse.masks import make_identity

F32 = mybir.dt.float32
BF16 = mybir.dt.bfloat16
U32 = mybir.dt.uint32
U8 = mybir.dt.uint8
FP8X4 = mybir.dt.float8_e4m3fn_x4
ACT = mybir.ActivationFunctionType
ALU = mybir.AluOpType
AX = mybir.AxisListType

P = 128
H = 16
HKV = 2
S = 1024
D = 128
HALF = S // 2
NT = S // P
NU = H * NT
NQ = NU // 4
SCALE = 1.0 / (D ** 0.5)
RSCALE = D ** 0.5
FLOPS = 2 * 2 * H * S * S * D


def copy_on_vector(i):
    return i == NU - 2 or (i % 4 == 3 and i < NU - 1)


def tile_deepseekv4attention_kernel(tc, query, key, value, attention_mask, sinks, out):
    nc = tc.nc
    with ExitStack() as ctx:
        const = ctx.enter_context(tc.tile_pool(name="const", bufs=1))
        qt_pool = ctx.enter_context(tc.tile_pool(name="qtp", bufs=4))
        e_pool = ctx.enter_context(tc.tile_pool(name="ep", bufs=4))
        et_pool = ctx.enter_context(tc.tile_pool(name="etp", bufs=3))
        c_pool = ctx.enter_context(tc.tile_pool(name="cp", bufs=3))
        small = ctx.enter_context(tc.tile_pool(name="small", bufs=4))
        o_pool = ctx.enter_context(tc.tile_pool(name="op", bufs=3))
        ps_s = ctx.enter_context(tc.psum_pool(name="ps_s", bufs=6))
        ps_t = ctx.enter_context(tc.psum_pool(name="ps_t", bufs=1))
        ps_x = ctx.enter_context(tc.psum_pool(name="ps_x", bufs=1))
        ctx.enter_context(tc.manual_schedule())

        q_v = query[0].rearrange("h (p t) d -> p h t d", t=NT)
        m_v = attention_mask[0, 0].rearrange("(p t) k -> p t k", t=NT)
        k_v = key[0].rearrange("g (a n e) d -> n g a e d", n=P, e=2)
        v_v = value[0].rearrange("g (a n z e) d -> e n g a z d", n=P // 2, z=2, e=2)
        o_v = out[0].rearrange("(p t) h d -> p t h d", t=NT)

        q_raw = const.tile([P, H, NT, D], BF16)
        mask_sb = const.tile([P, NT, S], BF16)
        mask_t = const.tile([P, NT, 8, P], F32)
        k_raw = const.tile([P, HKV, 4, 2, D], BF16)
        v_raw = const.tile([P, HKV, 4, 2, D], BF16)
        sink_bf = const.tile([P, H], BF16)
        sink_f = const.tile([P, H], F32)
        nsink = const.tile([P, H], F32)
        kt_sb = const.tile([P, HKV, S], BF16)
        v_codes = const.tile([P, HKV, 2 * D], U32, align_bytes=64)
        v_scales = const.tile([P, HKV, 2 * D], U8, align_bytes=64)
        v_grouped = const.tile([P, 2, D, 4], BF16, align_bytes=64)
        ident = const.tile([P, P], BF16)
        ident32 = const.tile([P, P], F32)

        make_identity(nc, ident[:])
        make_identity(nc, ident32[:])

        nc.sync.dma_start(out=k_raw[:, 0, 0:2], in_=k_v[:, 0, 0:2])
        nc.sync.dma_start(out=k_raw[:, 0, 2:4], in_=k_v[:, 0, 2:4])
        nc.sync.dma_start(out=q_raw[:, 0:4, 0, :], in_=q_v[:, 0:4, 0, :])
        nc.sync.dma_start(out=mask_sb[:, 0, 0:HALF], in_=m_v[:, 0, 0:HALF])
        nc.sync.dma_start(out=mask_sb[:, 0, HALF:S], in_=m_v[:, 0, HALF:S])
        nc.sync.dma_start(out=sink_bf[:], in_=sinks.partition_broadcast(P))
        nc.sync.dma_start(out=q_raw[:, 4:8, 0, :], in_=q_v[:, 4:8, 0, :])
        nc.sync.dma_start(out=k_raw[:, 1], in_=k_v[:, 1])
        nc.sync.dma_start(out=q_raw[:, 8:16, 0, :], in_=q_v[:, 8:16, 0, :])
        nc.sync.dma_start(out=mask_sb[:, 1, :], in_=m_v[:, 1, :])
        for g in range(HKV):
            for a in range(4):
                for e in range(2):
                    half = slice(P // 2 * e, P // 2 * e + P // 2)
                    nc.sync.dma_start(out=v_raw[half, g, a], in_=v_v[e, :, g, a])
        nc.sync.dma_start(out=q_raw[:, :, 1, :], in_=q_v[:, :, 1, :])
        for t in range(2, NT, 2):
            nc.sync.dma_start(out=mask_sb[:, t : t + 2, :], in_=m_v[:, t : t + 2, :])
            nc.sync.dma_start(out=q_raw[:, :, t : t + 2, :], in_=q_v[:, :, t : t + 2, :])

        nc.gpsimd.tensor_copy(out=sink_f[:], in_=sink_bf[:])
        nc.gpsimd.tensor_scalar(
            out=nsink[:], in0=sink_bf[:], scalar1=-1.0, scalar2=0.0, op0=ALU.mult, op1=ALU.add
        )

        x_ps = {}
        qt_sb = {}

        def prep_kt_pe(g, kt_ps):
            for a in range(NT):
                nc.tensor.transpose(out=kt_ps[:, a, :], in_=k_raw[:, g, a // 2, a % 2, :], identity=ident[:])
            x_ps["k%d" % g] = kt_ps[:]

        def prep_kt_copy(g):
            nc.scalar.copy(out=kt_sb[:, g, :], in_=x_ps["k%d" % g].rearrange("p a k -> p (a k)"))

        def prep_mask_pe(t, mp, w0, w1):
            pairs = mask_sb[:, t, :].bitcast(F32)
            for w in range(w0, w1):
                nc.tensor.transpose(out=mp[:, w - w0, :], in_=pairs[:, P * w : P * w + P], identity=ident32[:])
            x_ps["m%d_%d" % (t, w0)] = mp[:, 0 : w1 - w0, :]

        def prep_mask_copy(t, w0, w1, on_vector=False):
            pairs = x_ps["m%d_%d" % (t, w0)].rearrange("p w q -> p (w q)").bitcast(BF16)
            src = pairs.rearrange("p (w q e) -> p w e q", w=w1 - w0, e=2)
            dst = mask_t[:, t, 2 * w0 : 2 * w1, :].rearrange("p (w e) q -> p w e q", e=2)
            if on_vector:
                nc.vector.tensor_scalar(out=dst, in0=src, scalar1=RSCALE, scalar2=None, op0=ALU.mult)
            else:
                nc.scalar.activation(out=dst, in_=src, func=ACT.Copy, scale=RSCALE)

        def prep_v(g):
            nc.vector.tensor_copy(out=v_grouped[:], in_=v_raw[:, g].rearrange("p (c u) e d -> p c d (u e)", u=2))
            nc.vector.quantize_mx(
                out=v_codes[:, g, :].bitcast(FP8X4),
                scales=v_scales[:, g, :],
                in_=v_grouped[:].rearrange("p c d t -> p (c d t)"),
            )

        def prep_qt_pe(b, q_ps, j0=0, j1=8):
            t, octet = divmod(b, 2)
            for j in range(j0, j1):
                nc.tensor.transpose(out=q_ps[:, j % 4 if j1 - j0 == 4 else j, :], in_=q_raw[:, 8 * octet + j, t, :], identity=ident[:])
            x_ps["q%d" % b] = q_ps

        def prep_qt_copy(b, on_vector=False, j0=0, j1=8):
            if j0 == 0:
                qt = qt_pool.tile([P, 8, P], BF16, tag="qtsb")
                qt_sb[b] = qt
            dst, src = qt_sb[b][:, j0:j1, :], x_ps["q%d" % b][:, 0 : j1 - j0, :]
            if on_vector:
                nc.vector.tensor_copy(out=dst, in_=src)
            else:
                nc.scalar.copy(out=dst, in_=src)

        sc = {}
        nmax = {}
        ncap = {}
        negm = {}
        den = {}
        sdiff = {}
        dsum = {}
        rden = {}
        e_sb = {}
        tr_ps = {}
        et_sb = {}
        codes = {}
        scales = {}
        pv = {}
        o_sb = {}

        def where(i):
            t, r = divmod(i, H)
            hq, j = divmod(r, 4)
            return hq, t, j

        def qk(i):
            hq, t, j = where(i)
            g = (4 * hq + j) // (H // HKV)
            for c in range(2):
                s_t = ps_s.tile([P, HALF], F32, tag="sc")
                nc.tensor.matmul(
                    out=s_t[:],
                    lhsT=qt_sb[i // 8][:, i % 8, :],
                    rhs=kt_sb[:, g, HALF * c : HALF * c + HALF],
                    start=True,
                    stop=False,
                )
                sc[i, c] = s_t
            for a in range(8):
                c, a4 = divmod(a, 4)
                nc.tensor.matmul(
                    out=sc[i, c][:, P * a4 : P * a4 + P],
                    lhsT=mask_t[:, t, a, :],
                    rhs=ident32[:],
                    is_transpose=True,
                    start=False,
                    stop=(a4 == 3),
                )

        def rmax(i, c):
            n_t = small.tile([P, 1], F32, tag="nmax%d" % c, name="nm_t")
            nc.vector.tensor_reduce(out=n_t[:], in_=sc[i, c][:], axis=AX.X, op=ALU.max, negate=True)
            nmax[i, c] = n_t

        def tn(i, c):
            hq, t, j = where(i)
            h = 4 * hq + j
            if c == 0:
                if j == 0:
                    n4_t = small.tile([P, 4], F32, tag="negm")
                    negm[i // 4] = n4_t
                t_t = small.tile([P, 1], F32, tag="tmp")
                ncap[i] = t_t
                out, cap = t_t[:], nsink[:, h : h + 1]
            else:
                out, cap = negm[i // 4][:, j : j + 1], ncap[i][:]
            nc.gpsimd.tensor_scalar(
                out=out, in0=nmax[i, c][:], scalar1=SCALE, scalar2=cap, op0=ALU.mult, op1=ALU.min
            )

        def ex(i):
            j = i % 4
            if j == 0:
                den_t = small.tile([P, 4, 3], F32, tag="den")
                den[i // 4] = den_t
            e_t = e_pool.tile([P, S], BF16, tag="e")
            for c in range(2):
                nc.scalar.activation(
                    out=e_t[:, HALF * c : HALF * c + HALF],
                    in_=sc[i, c][:],
                    func=ACT.Exp,
                    bias=negm[i // 4][:, j : j + 1],
                    scale=SCALE,
                    accum_out=den[i // 4][:, j, c : c + 1],
                )
            e_sb[i] = e_t

        def sink_diff(quad):
            hq, t, jz = where(4 * quad)
            d_t = small.tile([P, 4], F32, tag="sdiff")
            nc.gpsimd.tensor_tensor(out=d_t[:], in0=negm[quad][:], in1=sink_f[:, 4 * hq : 4 * hq + 4], op=ALU.add)
            sdiff[quad] = d_t

        def sink_exp(quad):
            nc.scalar.activation(out=den[quad][:, :, 2], in_=sdiff[quad][:], func=ACT.Exp)

        def den_sum(quad):
            sum_t = small.tile([P, 4], F32, tag="esum")
            dsum_t = small.tile([P, 4], F32, tag="dsum")
            nc.gpsimd.tensor_tensor(out=sum_t[:], in0=den[quad][:, :, 0], in1=den[quad][:, :, 1], op=ALU.add)
            nc.gpsimd.tensor_tensor(out=dsum_t[:], in0=sum_t[:], in1=den[quad][:, :, 2], op=ALU.add)
            dsum[quad] = dsum_t

        def tr(i):
            if i < NU - 2:
                tr_t = ps_t.tile([P, 4, P], F32, tag="tr")
            else:
                tr_t = ps_s.tile([P, 4, P], F32, tag="sc")
            words = e_sb[i][:].bitcast(F32)
            for a in range(4):
                c, u = divmod(a, 2)
                nc.tensor.transpose(out=tr_t[:, 2 * u + c, :], in_=words[:, P * a : P * a + P], identity=ident32[:])
            tr_ps[i] = tr_t

        def p4(i):
            j = i % 4
            if j == 0:
                et_t = et_pool.tile([P, 8, P, 4], BF16, tag="et", align_bytes=64)
                et_sb[i // 4] = et_t
            et32 = et_sb[i // 4][:].rearrange("p c q t -> p (c q t)").bitcast(F32)
            dst = et32[:, 4 * P * j : 4 * P * (j + 1)].rearrange("p (n u) -> p n u", u=2)
            src = tr_ps[i][:].rearrange("p (u c) q -> p (c q) u", u=2)
            if copy_on_vector(i):
                nc.vector.tensor_copy(out=dst, in_=src)
            else:
                nc.scalar.copy(out=dst, in_=src)

        def quantise(i, n=2):
            quad, j = divmod(i, 4)
            j = j + 1 - n
            if j == 0:
                c_t = c_pool.tile([P, 8 * P], U32, tag="codes", align_bytes=64)
                sc_b = c_pool.tile([P, 8 * P], U8, tag="scales", align_bytes=64)
                codes[quad] = c_t
                scales[quad] = sc_b
            cols = slice(2 * P * j, 2 * P * (j + n))
            nc.vector.quantize_mx(
                out=codes[quad][:, cols].bitcast(FP8X4),
                scales=scales[quad][:, cols],
                in_=et_sb[quad][:, 2 * j : 2 * j + 2 * n].rearrange("p c q t -> p (c q t)"),
            )

        def mx(quad, j0=0, j1=4):
            if j0 == 0:
                pv_t = ps_x.tile([P, 4, D], F32, tag="x")
            else:
                pv_t = ps_s.tile([P, 4, D], F32, tag="sc")
            pv[quad] = pv_t
            hq = where(4 * quad)[0]
            for j in range(j0, j1):
                g = (4 * hq + j) // (H // HKV)
                for c in range(2):
                    cols = slice(P * (2 * j + c), P * (2 * j + c) + P)
                    vcols = slice(P * c, P * c + P)
                    nc.tensor.matmul_mx(
                        out=pv_t[:, j, :],
                        lhsT=codes[quad][:, cols].bitcast(FP8X4),
                        lhsT_scale=scales[quad][:, cols],
                        rhs=v_codes[:, g, vcols].bitcast(FP8X4),
                        rhs_scale=v_scales[:, g, vcols],
                        start=(c == 0),
                        stop=(c == 1),
                    )

        def recip(quad):
            r_t = small.tile([P, 4], F32, tag="rden")
            nc.vector.reciprocal(out=r_t[:], in_=dsum[quad][:])
            rden[quad] = r_t

        def p6(quad, j0=0, j1=4):
            hq, t, jz = where(4 * quad)
            if j0 == 0:
                o_t = o_pool.tile([P, 4, D], F32, tag="o")
                o_sb[quad] = o_t
            o_t = o_sb[quad]
            nc.vector.tensor_tensor(
                out=o_t[:, j0:j1, :],
                in0=pv[quad][:, j0:j1, :],
                in1=rden[quad][:, j0:j1].unsqueeze(2).to_broadcast([P, j1 - j0, D]),
                op=ALU.mult,
            )
            nc.sync.dma_start(out=o_v[:, t, 4 * hq + j0 : 4 * hq + j1, :], in_=o_t[:, j0:j1, :])

        head_ps = [ps_s.tile([P, 8, P], BF16, tag="sc", name="head_ps") for n in range(2)]
        mask_ps = [ps_s.tile([P, 4, P], F32, tag="sc", name="mask_ps") for n in range(2)]
        warm_ps = ps_x.tile([P, P], F32, tag="x")

        def warm(n):
            for k in range(n):
                nc.tensor.matmul(out=warm_ps[:], lhsT=ident[:], rhs=ident[:], start=True, stop=True)

        warm(18)
        prep_kt_pe(0, head_ps[0])
        prep_qt_pe(0, head_ps[1], 0, 4)
        prep_kt_copy(0)
        prep_qt_copy(0, True, 0, 4)
        prep_mask_pe(0, mask_ps[0], 0, 2)
        prep_mask_pe(0, mask_ps[1], 2, 4)
        prep_mask_copy(0, 0, 2)
        prep_mask_copy(0, 2, 4, on_vector=True)
        rest_ps = ps_x.tile([P, 8, P], BF16, tag="x")
        prep_qt_pe(0, rest_ps, 4, 8)
        prep_qt_copy(0, True, 4, 8)

        prep_at = {0: ("k", 1)}
        for n in range(1, NQ - 1):
            prep_at[4 * n - 3] = ("qm", n)

        def quad_at(i, lag):
            last = i - lag
            if 0 <= last < NU - 4 and last % 4 == 3:
                return last // 4
            return None

        def prep_copy(i):
            if i - 1 not in prep_at:
                return
            kind, n = prep_at[i - 1]
            if kind == "k":
                prep_kt_copy(n)
                return
            b, half = divmod(n + 1, 2)
            if b < NU // 8:
                prep_qt_copy(b, i > 8, 4 * half, 4 * half + 4)
            t, w = divmod(n - 1, 4)
            if t + 1 < NT:
                prep_mask_copy(t + 1, w, w + 1)

        for i in range(-1, NU + 3):
            q_d = quad_at(i, 1)
            q_s = quad_at(i, 2)
            q_m = quad_at(i, 3)
            q_r = quad_at(i, 4)
            q_mx1 = quad_at(i, 5)
            q_out = quad_at(i, 6)
            if 0 <= i - 3 < NU and not copy_on_vector(i - 3):
                p4(i - 3)
            if q_out is not None:
                p6(q_out)
            if 0 <= i - 4 < NU - 2 and i % 2 == 1:
                quantise(i - 4)
            if 0 <= i < NU:
                rmax(i, 0)
                tn(i, 0)
                rmax(i, 1)
                tn(i, 1)
            if 0 <= i - 3 < NU and copy_on_vector(i - 3):
                p4(i - 3)
            if i == NU + 1:
                quantise(NU - 2, 1)
            if q_r is not None:
                recip(q_r)
            if i in (3, 7):
                prep_v(0 if i == 3 else 1)
            if q_mx1 is not None:
                mx(q_mx1)
            if i + 1 < NU:
                qk(i + 1)
            if 0 <= i - 2 < NU:
                tr(i - 2)
            if 0 <= i - 1 < NU:
                ex(i - 1)
            prep_copy(i)
            if q_d is not None:
                sink_diff(q_d)
            if q_s is not None:
                sink_exp(q_s)
            if q_m is not None:
                den_sum(q_m)
            if i == NU:
                sink_diff(NQ - 1)
                sink_exp(NQ - 1)
                den_sum(NQ - 1)
            if i == NU + 2:
                mx(NQ - 1, 0, 3)
                recip(NQ - 1)
                quantise(NU - 1, 1)
                p6(NQ - 1, 0, 3)
                mx(NQ - 1, 3, 4)
                p6(NQ - 1, 3, 4)
            if i in prep_at:
                kind, n = prep_at[i]
                if kind == "k":
                    prep_ps = ps_x.tile([P, 8, P], BF16, tag="x")
                    prep_kt_pe(n, prep_ps)
                else:
                    prep_ps = ps_x.tile([P, 4, P], F32, tag="x")
                    b, half = divmod(n + 1, 2)
                    if b < NU // 8:
                        prep_qt_pe(b, prep_ps[:, 0:2].rearrange("p w q -> p (w q)").bitcast(BF16).rearrange("p (j q) -> p j q", q=P), 4 * half, 4 * half + 4)
                    t, w = divmod(n - 1, 4)
                    if t + 1 < NT:
                        prep_mask_pe(t + 1, prep_ps[:, 2:4], w, w + 1)
